import numpy as np
import ml_dtypes


def mxq(x, axis, fmt="e4m3"):
    dtype, down = {"e4m3": (ml_dtypes.float8_e4m3fn, 7), "e5m2": (ml_dtypes.float8_e5m2, 14)}[fmt]
    v = np.moveaxis(np.asarray(x, np.float32).astype(ml_dtypes.bfloat16).astype(np.float64), axis, -1)
    blocks = v.reshape(v.shape[:-1] + (-1, 32))
    amax = np.abs(blocks).max(-1, keepdims=True)
    byte = np.maximum(np.where(amax > 0, np.frexp(amax)[1] - 1 + 127, 0) - down, 1)
    scale = np.exp2(byte - 127.0)
    codes = (blocks / scale).astype(np.float32).astype(dtype).astype(np.float64)
    return np.moveaxis((codes * scale).reshape(v.shape), -1, axis)


WIDE = False


def mx_kscale(k):
    if not WIDE:
        return np.ones(k)
    levels = np.array([10, -10, 5, -5, 0])
    a = np.random.permutation(np.resize(levels, k // 512 * 4)).reshape(k // 512, 4)
    idx = np.arange(k)
    return np.exp2(a[idx // 512, idx % 128 // 32])


BF16 = ml_dtypes.bfloat16


def bf(x):
    return np.asarray(x, np.float32).astype(BF16)


def f64(x):
    return np.asarray(x).astype(np.float64)


C, H, W = 1024, 32, 32
N = H * W


def softmax_rows(s):
    e = np.exp(s - s.max(-1, keepdims=True))
    return e / e.sum(-1, keepdims=True)


def setup_inputs():
    s = mx_kscale(C)
    return {"score_f": bf(np.random.standard_normal((C, C)) * 2.0),
            "score_l": bf(np.random.standard_normal((C, C)) * 2.0),
            "x_m": bf(np.random.standard_normal((C, N)) * s[:, None]),
            "Wv": bf(np.random.standard_normal((C, C)) * 2.0 / np.sqrt(C) / s),
            "bv": bf(np.random.standard_normal(C) * 0.5),
            "gamma": bf(2.0 + 0.2 * np.random.standard_normal(1)),
            "x_f": bf(np.random.standard_normal((C, N))),
            "x_l": bf(np.random.standard_normal((C, N)))}


def reference(score_f, score_l, x_m, Wv, bv, gamma, x_f, x_l):
    att_f = mxq(softmax_rows(f64(score_f)), 1, "e4m3")
    att_l = mxq(softmax_rows(f64(score_l)), 1, "e4m3")
    v = mxq((mxq(f64(Wv), 1, "e4m3") @ mxq(f64(x_m), 0, "e4m3")) + f64(bv)[:, None], 0, "e4m3")
    o = (att_f @ v) + (att_l @ v)
    return f64(gamma) * o + (f64(x_l) + f64(x_f)) / 2

@@ -1,0 +1,255 @@
+from contextlib import ExitStack
+
+import concourse.mybir as mybir
+from concourse.masks import make_identity
+
+FP8X4 = mybir.dt.float8_e4m3fn_x4
+BF16 = mybir.dt.bfloat16
+F32 = mybir.dt.float32
+U32 = mybir.dt.uint32
+U8 = mybir.dt.uint8
+ALU = mybir.AluOpType
+ACT = mybir.ActivationFunctionType
+
+P = 128
+PACK = 4
+K_PASS = P * PACK
+C = 1024
+N = 1024
+PASSES = C // K_PASS
+ROW_TILES = C // P
+HALF = 512
+HALVES = N // HALF
+CHUNK = 128
+AHEAD = 2
+
+FLOPS = 3 * 2 * C * C * N
+
+
+def tile_coatten2_pb_kernel(tc, score_f, score_l, x_m, Wv, bv, gamma, x_f, x_l, out):
+    nc = tc.nc
+    with ExitStack() as ctx:
+        const = ctx.enter_context(tc.tile_pool(name="const", bufs=1))
+        keep = ctx.enter_context(tc.tile_pool(name="keep", bufs=1))
+        big = ctx.enter_context(tc.tile_pool(name="big", bufs=4))
+        work = ctx.enter_context(tc.tile_pool(name="work", bufs=3))
+        psum_turn = ctx.enter_context(tc.psum_pool(name="psum_turn", bufs=2))
+        psum_one = ctx.enter_context(tc.psum_pool(name="psum_one", bufs=3))
+        psum_two = ctx.enter_context(tc.psum_pool(name="psum_two", bufs=3))
+
+        ident = const.tile([P, P], F32, name="ident")
+        make_identity(nc, ident[:])
+        half_ident = const.tile([P, P], BF16, name="half_ident")
+        nc.vector.tensor_scalar(
+            out=half_ident[:], in0=ident[:], scalar1=0.5, scalar2=None, op0=ALU.mult
+        )
+        bias_bf = const.tile([P, PASSES * 2, 2], BF16, name="bias_bf")
+        nc.scalar.dma_start(out=bias_bf[:], in_=bv.rearrange("(a p e) -> p a e", p=P, e=2))
+        bias = const.tile([P, PASSES * PACK], F32, name="bias")
+        nc.vector.tensor_copy(out=bias[:], in_=bias_bf[:].rearrange("p a e -> p (a e)"))
+        gain_bf = const.tile([P, 1], BF16, name="gain_bf")
+        nc.scalar.dma_start(out=gain_bf[:], in_=gamma.partition_broadcast(P))
+        gain = const.tile([P, 1], F32, name="gain")
+        nc.vector.tensor_copy(out=gain[:], in_=gain_bf[:])
+
+        scores = {"f": score_f, "l": score_l}
+        score_sb = {}
+
+        def load_scores(r):
+            for x in ("f", "l"):
+                score_sb[x, r] = keep.tile([P, C], BF16, name="score_%s%d" % (x, r))
+                nc.sync.dma_start(out=score_sb[x, r][:], in_=scores[x][r * P : (r + 1) * P, :])
+
+        def load_paired_rows(src, name):
+            tiles = []
+            for g in range(PASSES):
+                t = big.tile([P, PACK, src.shape[1]], BF16, name="%s%d" % (name, g), tag="big")
+                for u in range(2):
+                    rows = src[g * K_PASS + u * 2 * P : g * K_PASS + (u + 1) * 2 * P, :]
+                    nc.sync.dma_start(
+                        out=t[:, 2 * u : 2 * u + 2, :], in_=rows.rearrange("(p e) n -> p e n", e=2)
+                    )
+                tiles.append(t)
+            return tiles
+
+        for r in range(AHEAD):
+            load_scores(r)
+        xm_raw = load_paired_rows(x_m, "xm_raw")
+        wv_raw = load_paired_rows(Wv, "wv_raw")
+        for r in range(AHEAD, ROW_TILES):
+            load_scores(r)
+
+        neg_max = const.tile([P, 2 * ROW_TILES], F32, name="neg_max")
+        row_sum = const.tile([P, 2 * ROW_TILES], F32, name="row_sum")
+        inv_sum = const.tile([P, 2 * ROW_TILES], F32, name="inv_sum")
+        att_codes = {}
+        att_scales = {}
+
+        def softmax_tile(r):
+            att_grouped = work.tile([P, 2 * C], BF16, name="att_grouped", align_bytes=64)
+            grouped_words = att_grouped[:].bitcast(F32).rearrange(
+                "p (x g c u) -> p x g c u", x=2, g=PASSES, u=2
+            )
+            for i, x in enumerate(("f", "l")):
+                col = slice(2 * r + i, 2 * r + i + 1)
+                expo = work.tile([P, C], F32, name="expo")
+                nc.vector.tensor_scalar(
+                    out=expo[:, 0 : C // 2].bitcast(BF16),
+                    in0=score_sb[x, r][:],
+                    scalar1=-1.0,
+                    scalar2=None,
+                    op0=ALU.mult,
+                    op1=ALU.min,
+                    accum_out=neg_max[:, col],
+                )
+                nc.scalar.activation(
+                    out=expo[:],
+                    in_=score_sb[x, r][:],
+                    func=ACT.Exp,
+                    bias=neg_max[:, col],
+                    scale=1.0,
+                    accum_out=row_sum[:, col],
+                )
+                nc.vector.reciprocal(out=inv_sum[:, col], in_=row_sum[:, col])
+                att = work.tile([P, C], BF16, name="att")
+                if x == "f":
+                    nc.vector.tensor_scalar(
+                        out=att[:], in0=expo[:], scalar1=inv_sum[:, col], scalar2=None, op0=ALU.mult
+                    )
+                else:
+                    nc.scalar.activation(out=att[:], in_=expo[:], func=ACT.Copy, scale=inv_sum[:, col])
+                att_words = att[:].bitcast(F32)
+                turned = psum_turn.tile([P, PASSES, 2, P], F32, name="turned")
+                for g in range(PASSES):
+                    for u in range(2):
+                        first = (2 * g + u) * P
+                        nc.tensor.transpose(turned[:, g, u, :], att_words[:, first : first + P], ident[:])
+                nc.scalar.copy(out=grouped_words[:, i], in_=turned[:].rearrange("p g u c -> p g c u"))
+            att_codes[r] = keep.tile([P, 2 * PASSES * P], U32, name="att_codes%d" % r, align_bytes=64)
+            att_scales[r] = keep.tile([P, 2 * PASSES * P], U8, name="att_scales%d" % r, align_bytes=64)
+            nc.vector.quantize_mx(
+                out=att_codes[r][:].bitcast(FP8X4), scales=att_scales[r][:], in_=att_grouped[:]
+            )
+
+        for r in range(AHEAD):
+            softmax_tile(r)
+
+        xm_codes = keep.tile([P, PASSES, N], U32, name="xm_codes", align_bytes=64)
+        xm_scales = keep.tile([P, PASSES, N], U8, name="xm_scales", align_bytes=64)
+        for h in range(HALVES):
+            cols = slice(h * HALF, (h + 1) * HALF)
+            for g in range(PASSES):
+                xm_grouped = work.tile([P, HALF, PACK], BF16, name="xm_grouped", align_bytes=64)
+                nc.vector.tensor_copy(
+                    out=xm_grouped[:].rearrange("p (c i) t -> p c t i", i=4),
+                    in_=xm_raw[g][:, :, cols].rearrange("p t (c i) -> p c t i", i=4),
+                )
+                nc.vector.quantize_mx(
+                    out=xm_codes[:, g, cols].bitcast(FP8X4),
+                    scales=xm_scales[:, g, cols],
+                    in_=xm_grouped[:].rearrange("p n t -> p (n t)"),
+                )
+
+        wv_codes = []
+        wv_scales = []
+        for s in range(PASSES):
+            wv_grouped = keep.tile([P, PASSES * K_PASS * PACK], BF16, name="wv_grouped%d" % s, align_bytes=64)
+            grouped_words = wv_grouped[:].bitcast(F32).rearrange("p (g d u) -> p g d u", g=PASSES, u=2)
+            wv_words = wv_raw[s][:].rearrange("p t k -> p (t k)").bitcast(F32)
+            for t in range(PACK):
+                turned = psum_one.tile([P, PASSES, 2, P], F32, name="wv_turned", tag="one")
+                for g in range(PASSES):
+                    for u in range(2):
+                        first = t * (C // 2) + (2 * g + u) * P
+                        nc.tensor.transpose(turned[:, g, u, :], wv_words[:, first : first + P], ident[:])
+                nc.scalar.copy(
+                    out=grouped_words[:, :, t * P : (t + 1) * P, :],
+                    in_=turned[:].rearrange("p g u d -> p g d u"),
+                )
+            wv_codes.append(keep.tile([P, PASSES, K_PASS], U32, name="wv_codes%d" % s, align_bytes=64))
+            wv_scales.append(keep.tile([P, PASSES, K_PASS], U8, name="wv_scales%d" % s, align_bytes=64))
+            nc.vector.quantize_mx(
+                out=wv_codes[s][:].rearrange("p g d -> p (g d)").bitcast(FP8X4),
+                scales=wv_scales[s][:].rearrange("p g d -> p (g d)"),
+                in_=wv_grouped[:],
+            )
+
+        xf_sb = []
+        xl_sb = []
+        for a in range(ROW_TILES // PACK):
+            xf_sb.append(big.tile([P, PACK, N], BF16, name="xf_sb%d" % a, tag="big"))
+            xl_sb.append(big.tile([P, PACK, N], BF16, name="xl_sb%d" % a, tag="big"))
+            for b in range(PACK):
+                rows = slice((a * PACK + b) * P, (a * PACK + b + 1) * P)
+                nc.sync.dma_start(out=xf_sb[a][:, b, :], in_=x_f[rows, :])
+                nc.sync.dma_start(out=xl_sb[a][:, b, :], in_=x_l[rows, :])
+
+        v_codes = keep.tile([P, PASSES, N], U32, name="v_codes", align_bytes=64)
+        v_scales = keep.tile([P, PASSES, N], U8, name="v_scales", align_bytes=64)
+        for h in range(HALVES):
+            for s in range(PASSES):
+                v_grouped = work.tile([P, HALF, PACK], BF16, name="v_grouped", align_bytes=64)
+                for j in range(HALF // CHUNK):
+                    pix = slice(h * HALF + j * CHUNK, h * HALF + (j + 1) * CHUNK)
+                    v_acc = psum_one.tile([P, PACK, CHUNK], F32, name="v_acc", tag="one")
+                    for t in range(PACK):
+                        for g in range(PASSES):
+                            nc.tensor.matmul_mx(
+                                out=v_acc[:, t, :],
+                                lhsT=wv_codes[s][:, g, t * P : (t + 1) * P].bitcast(FP8X4),
+                                lhsT_scale=wv_scales[s][:, g, t * P : (t + 1) * P],
+                                rhs=xm_codes[:, g, pix].bitcast(FP8X4),
+                                rhs_scale=xm_scales[:, g, pix],
+                                start=(g == 0),
+                                stop=(g == PASSES - 1),
+                            )
+                    nc.vector.tensor_tensor(
+                        out=v_grouped[:, j * CHUNK : (j + 1) * CHUNK, :],
+                        in0=v_acc[:].rearrange("p t n -> p n t"),
+                        in1=bias[:, s * PACK : (s + 1) * PACK].unsqueeze(1).to_broadcast([P, CHUNK, PACK]),
+                        op=ALU.add,
+                    )
+                cols = slice(h * HALF, (h + 1) * HALF)
+                nc.vector.quantize_mx(
+                    out=v_codes[:, s, cols].bitcast(FP8X4),
+                    scales=v_scales[:, s, cols],
+                    in_=v_grouped[:].rearrange("p n t -> p (n t)"),
+                )
+
+        for r in range(ROW_TILES):
+            if r + AHEAD < ROW_TILES:
+                softmax_tile(r + AHEAD)
+            mean = work.tile([P, N], F32, name="mean")
+            result = work.tile([P, N], F32, name="result")
+            for h in range(HALVES):
+                cols = slice(h * HALF, (h + 1) * HALF)
+                mean_acc = psum_two.tile([P, HALF], F32, name="mean_acc", tag="two")
+                nc.tensor.matmul(
+                    out=mean_acc[:], lhsT=half_ident[:], rhs=xl_sb[r // PACK][:, r % PACK, cols],
+                    start=True, stop=False,
+                )
+                nc.tensor.matmul(
+                    out=mean_acc[:], lhsT=half_ident[:], rhs=xf_sb[r // PACK][:, r % PACK, cols],
+                    start=False, stop=True,
+                )
+                nc.scalar.copy(out=mean[:, cols], in_=mean_acc[:])
+            for h in range(HALVES):
+                cols = slice(h * HALF, (h + 1) * HALF)
+                o_acc = psum_two.tile([P, HALF], F32, name="o_acc", tag="two")
+                for i in range(2):
+                    for g in range(PASSES):
+                        block = slice((i * PASSES + g) * P, (i * PASSES + g + 1) * P)
+                        nc.tensor.matmul_mx(
+                            out=o_acc[:],
+                            lhsT=att_codes[r][:, block].bitcast(FP8X4),
+                            lhsT_scale=att_scales[r][:, block],
+                            rhs=v_codes[:, g, cols].bitcast(FP8X4),
+                            rhs_scale=v_scales[:, g, cols],
+                            start=(i == 0 and g == 0),
+                            stop=(i == 1 and g == PASSES - 1),
+                        )
+                nc.vector.scalar_tensor_tensor(
+                    out=result[:, cols], in0=o_acc[:], scalar=gain[:, 0:1], in1=mean[:, cols],
+                    op0=ALU.mult, op1=ALU.add,
+                )
+            nc.sync.dma_start(out=out[r * P : (r + 1) * P, :], in_=result[:])

@@ -20,7 +20,6 @@ PASSES = C // K_PASS
 ROW_TILES = C // P
 HALF = 512
 HALVES = N // HALF
-CHUNK = 128
 AHEAD = 2
 
 FLOPS = 3 * 2 * C * C * N
@@ -60,24 +59,102 @@ def tile_coatten2_pb_kernel(tc, score_f, score_l, x_m, Wv, bv, gamma, x_f, x_l, 
                 score_sb[x, r] = keep.tile([P, C], BF16, name="score_%s%d" % (x, r))
                 nc.sync.dma_start(out=score_sb[x, r][:], in_=scores[x][r * P : (r + 1) * P, :])
 
-        def load_paired_rows(src, name):
-            tiles = []
-            for g in range(PASSES):
-                t = big.tile([P, PACK, src.shape[1]], BF16, name="%s%d" % (name, g), tag="big")
-                for u in range(2):
-                    rows = src[g * K_PASS + u * 2 * P : g * K_PASS + (u + 1) * 2 * P, :]
-                    nc.sync.dma_start(
-                        out=t[:, 2 * u : 2 * u + 2, :], in_=rows.rearrange("(p e) n -> p e n", e=2)
-                    )
-                tiles.append(t)
-            return tiles
+        def load_paired_rows(src, g, name):
+            t = big.tile([P, PACK, src.shape[1]], BF16, name="%s%d" % (name, g), tag="big")
+            for u in range(2):
+                rows = src[g * K_PASS + u * 2 * P : g * K_PASS + (u + 1) * 2 * P, :]
+                nc.sync.dma_start(
+                    out=t[:, 2 * u : 2 * u + 2, :], in_=rows.rearrange("(p e) n -> p e n", e=2)
+                )
+            return t
 
         for r in range(AHEAD):
             load_scores(r)
-        xm_raw = load_paired_rows(x_m, "xm_raw")
-        wv_raw = load_paired_rows(Wv, "wv_raw")
+        wv_raw = [load_paired_rows(Wv, 0, "wv_raw")]
+        xm_raw = [load_paired_rows(x_m, g, "xm_raw") for g in range(PASSES)]
+        wv_raw.append(load_paired_rows(Wv, 1, "wv_raw"))
         for r in range(AHEAD, ROW_TILES):
             load_scores(r)
+
+        wv_codes = {}
+        wv_scales = {}
+
+        def prepare_wv(s):
+            wv_grouped = keep.tile([P, PASSES * K_PASS * PACK], BF16, name="wv_grouped%d" % s, align_bytes=64)
+            grouped_words = wv_grouped[:].bitcast(F32).rearrange("p (g d u) -> p g d u", g=PASSES, u=2)
+            wv_words = wv_raw[s][:].rearrange("p t k -> p (t k)").bitcast(F32)
+            for t in range(PACK):
+                turned = psum_one.tile([P, PASSES, 2, P], F32, name="wv_turned", tag="one")
+                for g in range(PASSES):
+                    for u in range(2):
+                        first = t * (C // 2) + (2 * g + u) * P
+                        nc.tensor.transpose(turned[:, g, u, :], wv_words[:, first : first + P], ident[:])
+                nc.scalar.copy(
+                    out=grouped_words[:, :, t * P : (t + 1) * P, :],
+                    in_=turned[:].rearrange("p g u d -> p g d u"),
+                )
+            wv_codes[s] = keep.tile([P, PASSES, K_PASS], U32, name="wv_codes%d" % s, align_bytes=64)
+            wv_scales[s] = keep.tile([P, PASSES, K_PASS], U8, name="wv_scales%d" % s, align_bytes=64)
+            nc.vector.quantize_mx(
+                out=wv_codes[s][:].rearrange("p g d -> p (g d)").bitcast(FP8X4),
+                scales=wv_scales[s][:].rearrange("p g d -> p (g d)"),
+                in_=wv_grouped[:],
+            )
+
+        xm_codes = keep.tile([P, PASSES, N], U32, name="xm_codes", align_bytes=64)
+        xm_scales = keep.tile([P, PASSES, N], U8, name="xm_scales", align_bytes=64)
+
+        def regroup(dst, src):
+            nc.vector.tensor_copy(
+                out=dst.rearrange("p (c i) t -> p c t i", i=4),
+                in_=src.rearrange("p t (c i) -> p c t i", i=4),
+            )
+
+        def prepare_xm(h):
+            cols = slice(h * HALF, (h + 1) * HALF)
+            grouped = []
+            for g in range(PASSES):
+                grouped.append(work.tile([P, HALF, PACK], BF16, name="xm_grouped", align_bytes=64))
+                regroup(grouped[g][:], xm_raw[g][:, :, cols])
+            for g in range(PASSES):
+                nc.vector.quantize_mx(
+                    out=xm_codes[:, g, cols].bitcast(FP8X4),
+                    scales=xm_scales[:, g, cols],
+                    in_=grouped[g][:].rearrange("p n t -> p (n t)"),
+                )
+
+        v_codes = keep.tile([P, PASSES, N], U32, name="v_codes", align_bytes=64)
+        v_scales = keep.tile([P, PASSES, N], U8, name="v_scales", align_bytes=64)
+
+        def stage_one(h, s):
+            cols = slice(h * HALF, (h + 1) * HALF)
+            v_rows = work.tile([P, PACK, HALF], BF16, name="v_rows")
+            for t in range(PACK):
+                v_acc = psum_one.tile([P, HALF], F32, name="v_acc", tag="one")
+                for g in range(PASSES):
+                    nc.tensor.matmul_mx(
+                        out=v_acc[:],
+                        lhsT=wv_codes[s][:, g, t * P : (t + 1) * P].bitcast(FP8X4),
+                        lhsT_scale=wv_scales[s][:, g, t * P : (t + 1) * P],
+                        rhs=xm_codes[:, g, cols].bitcast(FP8X4),
+                        rhs_scale=xm_scales[:, g, cols],
+                        start=(g == 0),
+                        stop=(g == PASSES - 1),
+                    )
+                nc.scalar.activation(
+                    out=v_rows[:, t, :],
+                    in_=v_acc[:],
+                    func=ACT.Identity,
+                    bias=bias[:, s * PACK + t : s * PACK + t + 1],
+                    scale=1.0,
+                )
+            v_grouped = work.tile([P, HALF, PACK], BF16, name="v_grouped", align_bytes=64)
+            regroup(v_grouped[:], v_rows[:])
+            nc.vector.quantize_mx(
+                out=v_codes[:, s, cols].bitcast(FP8X4),
+                scales=v_scales[:, s, cols],
+                in_=v_grouped[:].rearrange("p n t -> p (n t)"),
+            )
 
         neg_max = const.tile([P, 2 * ROW_TILES], F32, name="neg_max")
         row_sum = const.tile([P, 2 * ROW_TILES], F32, name="row_sum")
@@ -112,12 +189,9 @@ def tile_coatten2_pb_kernel(tc, score_f, score_l, x_m, Wv, bv, gamma, x_f, x_l, 
                 )
                 nc.vector.reciprocal(out=inv_sum[:, col], in_=row_sum[:, col])
                 att = work.tile([P, C], BF16, name="att")
-                if x == "f":
-                    nc.vector.tensor_scalar(
-                        out=att[:], in0=expo[:], scalar1=inv_sum[:, col], scalar2=None, op0=ALU.mult
-                    )
-                else:
-                    nc.scalar.activation(out=att[:], in_=expo[:], func=ACT.Copy, scale=inv_sum[:, col])
+                nc.vector.tensor_scalar(
+                    out=att[:], in0=expo[:], scalar1=inv_sum[:, col], scalar2=None, op0=ALU.mult
+                )
                 att_words = att[:].bitcast(F32)
                 turned = psum_turn.tile([P, PASSES, 2, P], F32, name="turned")
                 for g in range(PASSES):
@@ -131,96 +205,20 @@ def tile_coatten2_pb_kernel(tc, score_f, score_l, x_m, Wv, bv, gamma, x_f, x_l, 
                 out=att_codes[r][:].bitcast(FP8X4), scales=att_scales[r][:], in_=att_grouped[:]
             )
 
-        for r in range(AHEAD):
-            softmax_tile(r)
-
-        xm_codes = keep.tile([P, PASSES, N], U32, name="xm_codes", align_bytes=64)
-        xm_scales = keep.tile([P, PASSES, N], U8, name="xm_scales", align_bytes=64)
-        for h in range(HALVES):
-            cols = slice(h * HALF, (h + 1) * HALF)
-            for g in range(PASSES):
-                xm_grouped = work.tile([P, HALF, PACK], BF16, name="xm_grouped", align_bytes=64)
-                nc.vector.tensor_copy(
-                    out=xm_grouped[:].rearrange("p (c i) t -> p c t i", i=4),
-                    in_=xm_raw[g][:, :, cols].rearrange("p t (c i) -> p c t i", i=4),
-                )
-                nc.vector.quantize_mx(
-                    out=xm_codes[:, g, cols].bitcast(FP8X4),
-                    scales=xm_scales[:, g, cols],
-                    in_=xm_grouped[:].rearrange("p n t -> p (n t)"),
-                )
-
-        wv_codes = []
-        wv_scales = []
-        for s in range(PASSES):
-            wv_grouped = keep.tile([P, PASSES * K_PASS * PACK], BF16, name="wv_grouped%d" % s, align_bytes=64)
-            grouped_words = wv_grouped[:].bitcast(F32).rearrange("p (g d u) -> p g d u", g=PASSES, u=2)
-            wv_words = wv_raw[s][:].rearrange("p t k -> p (t k)").bitcast(F32)
-            for t in range(PACK):
-                turned = psum_one.tile([P, PASSES, 2, P], F32, name="wv_turned", tag="one")
-                for g in range(PASSES):
-                    for u in range(2):
-                        first = t * (C // 2) + (2 * g + u) * P
-                        nc.tensor.transpose(turned[:, g, u, :], wv_words[:, first : first + P], ident[:])
-                nc.scalar.copy(
-                    out=grouped_words[:, :, t * P : (t + 1) * P, :],
-                    in_=turned[:].rearrange("p g u d -> p g d u"),
-                )
-            wv_codes.append(keep.tile([P, PASSES, K_PASS], U32, name="wv_codes%d" % s, align_bytes=64))
-            wv_scales.append(keep.tile([P, PASSES, K_PASS], U8, name="wv_scales%d" % s, align_bytes=64))
-            nc.vector.quantize_mx(
-                out=wv_codes[s][:].rearrange("p g d -> p (g d)").bitcast(FP8X4),
-                scales=wv_scales[s][:].rearrange("p g d -> p (g d)"),
-                in_=wv_grouped[:],
-            )
-
         xf_sb = []
         xl_sb = []
-        for a in range(ROW_TILES // PACK):
-            xf_sb.append(big.tile([P, PACK, N], BF16, name="xf_sb%d" % a, tag="big"))
-            xl_sb.append(big.tile([P, PACK, N], BF16, name="xl_sb%d" % a, tag="big"))
-            for b in range(PACK):
-                rows = slice((a * PACK + b) * P, (a * PACK + b + 1) * P)
-                nc.sync.dma_start(out=xf_sb[a][:, b, :], in_=x_f[rows, :])
-                nc.sync.dma_start(out=xl_sb[a][:, b, :], in_=x_l[rows, :])
 
-        v_codes = keep.tile([P, PASSES, N], U32, name="v_codes", align_bytes=64)
-        v_scales = keep.tile([P, PASSES, N], U8, name="v_scales", align_bytes=64)
-        for h in range(HALVES):
-            for s in range(PASSES):
-                v_grouped = work.tile([P, HALF, PACK], BF16, name="v_grouped", align_bytes=64)
-                for j in range(HALF // CHUNK):
-                    pix = slice(h * HALF + j * CHUNK, h * HALF + (j + 1) * CHUNK)
-                    v_acc = psum_one.tile([P, PACK, CHUNK], F32, name="v_acc", tag="one")
-                    for t in range(PACK):
-                        for g in range(PASSES):
-                            nc.tensor.matmul_mx(
-                                out=v_acc[:, t, :],
-                                lhsT=wv_codes[s][:, g, t * P : (t + 1) * P].bitcast(FP8X4),
-                                lhsT_scale=wv_scales[s][:, g, t * P : (t + 1) * P],
-                                rhs=xm_codes[:, g, pix].bitcast(FP8X4),
-                                rhs_scale=xm_scales[:, g, pix],
-                                start=(g == 0),
-                                stop=(g == PASSES - 1),
-                            )
-                    nc.vector.tensor_tensor(
-                        out=v_grouped[:, j * CHUNK : (j + 1) * CHUNK, :],
-                        in0=v_acc[:].rearrange("p t n -> p n t"),
-                        in1=bias[:, s * PACK : (s + 1) * PACK].unsqueeze(1).to_broadcast([P, CHUNK, PACK]),
-                        op=ALU.add,
-                    )
-                cols = slice(h * HALF, (h + 1) * HALF)
-                nc.vector.quantize_mx(
-                    out=v_codes[:, s, cols].bitcast(FP8X4),
-                    scales=v_scales[:, s, cols],
-                    in_=v_grouped[:].rearrange("p n t -> p (n t)"),
-                )
+        def load_frames():
+            for a in range(ROW_TILES // PACK):
+                xf_sb.append(big.tile([P, PACK, N], BF16, name="xf_sb%d" % a, tag="big"))
+                xl_sb.append(big.tile([P, PACK, N], BF16, name="xl_sb%d" % a, tag="big"))
+                for b in range(PACK):
+                    rows = slice((a * PACK + b) * P, (a * PACK + b + 1) * P)
+                    nc.sync.dma_start(out=xf_sb[a][:, b, :], in_=x_f[rows, :])
+                    nc.sync.dma_start(out=xl_sb[a][:, b, :], in_=x_l[rows, :])
 
-        for r in range(ROW_TILES):
-            if r + AHEAD < ROW_TILES:
-                softmax_tile(r + AHEAD)
+        def stage_two(r):
             mean = work.tile([P, N], F32, name="mean")
-            result = work.tile([P, N], F32, name="result")
             for h in range(HALVES):
                 cols = slice(h * HALF, (h + 1) * HALF)
                 mean_acc = psum_two.tile([P, HALF], F32, name="mean_acc", tag="two")
@@ -248,8 +246,24 @@ def tile_coatten2_pb_kernel(tc, score_f, score_l, x_m, Wv, bv, gamma, x_f, x_l, 
                             start=(i == 0 and g == 0),
                             stop=(i == 1 and g == PASSES - 1),
                         )
+                result = work.tile([P, HALF], F32, name="result")
                 nc.vector.scalar_tensor_tensor(
-                    out=result[:, cols], in0=o_acc[:], scalar=gain[:, 0:1], in1=mean[:, cols],
+                    out=result[:], in0=o_acc[:], scalar=gain[:, 0:1], in1=mean[:, cols],
                     op0=ALU.mult, op1=ALU.add,
                 )
-            nc.sync.dma_start(out=out[r * P : (r + 1) * P, :], in_=result[:])
+                nc.sync.dma_start(out=out[r * P : (r + 1) * P, cols], in_=result[:])
+
+        prepare_wv(0)
+        for h in range(HALVES):
+            prepare_xm(h)
+        prepare_wv(1)
+        load_frames()
+        for h in range(HALVES):
+            for s in range(PASSES):
+                stage_one(h, s)
+        for r in range(AHEAD):
+            softmax_tile(r)
+        for r in range(ROW_TILES):
+            if r + AHEAD < ROW_TILES:
+                softmax_tile(r + AHEAD)
+            stage_two(r)

@@ -32,9 +32,10 @@ def tile_coatten2_pb_kernel(tc, score_f, score_l, x_m, Wv, bv, gamma, x_f, x_l, 
         keep = ctx.enter_context(tc.tile_pool(name="keep", bufs=1))
         big = ctx.enter_context(tc.tile_pool(name="big", bufs=4))
         work = ctx.enter_context(tc.tile_pool(name="work", bufs=3))
+        long_work = ctx.enter_context(tc.tile_pool(name="long_work", bufs=4))
         psum_turn = ctx.enter_context(tc.psum_pool(name="psum_turn", bufs=2))
-        psum_one = ctx.enter_context(tc.psum_pool(name="psum_one", bufs=3))
-        psum_two = ctx.enter_context(tc.psum_pool(name="psum_two", bufs=3))
+        psum_acc = ctx.enter_context(tc.psum_pool(name="psum_acc", bufs=4))
+        psum_mean = ctx.enter_context(tc.psum_pool(name="psum_mean", bufs=2))
 
         ident = const.tile([P, P], F32, name="ident")
         make_identity(nc, ident[:])
@@ -84,7 +85,7 @@ def tile_coatten2_pb_kernel(tc, score_f, score_l, x_m, Wv, bv, gamma, x_f, x_l, 
             grouped_words = wv_grouped[:].bitcast(F32).rearrange("p (g d u) -> p g d u", g=PASSES, u=2)
             wv_words = wv_raw[s][:].rearrange("p t k -> p (t k)").bitcast(F32)
             for t in range(PACK):
-                turned = psum_one.tile([P, PASSES, 2, P], F32, name="wv_turned", tag="one")
+                turned = psum_acc.tile([P, PASSES, 2, P], F32, name="wv_turned", tag="acc")
                 for g in range(PASSES):
                     for u in range(2):
                         first = t * (C // 2) + (2 * g + u) * P
@@ -130,7 +131,7 @@ def tile_coatten2_pb_kernel(tc, score_f, score_l, x_m, Wv, bv, gamma, x_f, x_l, 
             cols = slice(h * HALF, (h + 1) * HALF)
             v_rows = work.tile([P, PACK, HALF], BF16, name="v_rows")
             for t in range(PACK):
-                v_acc = psum_one.tile([P, HALF], F32, name="v_acc", tag="one")
+                v_acc = psum_acc.tile([P, HALF], F32, name="v_acc", tag="acc")
                 for g in range(PASSES):
                     nc.tensor.matmul_mx(
                         out=v_acc[:],
@@ -159,54 +160,74 @@ def tile_coatten2_pb_kernel(tc, score_f, score_l, x_m, Wv, bv, gamma, x_f, x_l, 
         neg_max = const.tile([P, 2 * ROW_TILES], F32, name="neg_max")
         row_sum = const.tile([P, 2 * ROW_TILES], F32, name="row_sum")
         inv_sum = const.tile([P, 2 * ROW_TILES], F32, name="inv_sum")
+        maps = ("f", "l")
+        expo = {}
+        turned = {}
         att_codes = {}
         att_scales = {}
 
-        def softmax_tile(r):
-            att_grouped = work.tile([P, 2 * C], BF16, name="att_grouped", align_bytes=64)
-            grouped_words = att_grouped[:].bitcast(F32).rearrange(
-                "p (x g c u) -> p x g c u", x=2, g=PASSES, u=2
+        def row_max(r, i):
+            expo[r, i] = long_work.tile([P, C], F32, name="expo")
+            nc.vector.tensor_scalar(
+                out=expo[r, i][:, 0 : C // 2].bitcast(BF16),
+                in0=score_sb[maps[i], r][:],
+                scalar1=-1.0,
+                scalar2=None,
+                op0=ALU.mult,
+                op1=ALU.min,
+                accum_out=neg_max[:, 2 * r + i : 2 * r + i + 1],
             )
-            for i, x in enumerate(("f", "l")):
+
+        def exponentials(r):
+            for i in range(2):
                 col = slice(2 * r + i, 2 * r + i + 1)
-                expo = work.tile([P, C], F32, name="expo")
-                nc.vector.tensor_scalar(
-                    out=expo[:, 0 : C // 2].bitcast(BF16),
-                    in0=score_sb[x, r][:],
-                    scalar1=-1.0,
-                    scalar2=None,
-                    op0=ALU.mult,
-                    op1=ALU.min,
-                    accum_out=neg_max[:, col],
-                )
                 nc.scalar.activation(
-                    out=expo[:],
-                    in_=score_sb[x, r][:],
+                    out=expo[r, i][:],
+                    in_=score_sb[maps[i], r][:],
                     func=ACT.Exp,
                     bias=neg_max[:, col],
                     scale=1.0,
                     accum_out=row_sum[:, col],
                 )
-                nc.vector.reciprocal(out=inv_sum[:, col], in_=row_sum[:, col])
-                att = work.tile([P, C], BF16, name="att")
+
+        def scale_and_turn(r):
+            both = slice(2 * r, 2 * r + 2)
+            nc.vector.reciprocal(out=inv_sum[:, both], in_=row_sum[:, both])
+            att = []
+            for i in range(2):
+                att.append(work.tile([P, C], BF16, name="att"))
                 nc.vector.tensor_scalar(
-                    out=att[:], in0=expo[:], scalar1=inv_sum[:, col], scalar2=None, op0=ALU.mult
+                    out=att[i][:], in0=expo[r, i][:], scalar1=inv_sum[:, 2 * r + i : 2 * r + i + 1],
+                    scalar2=None, op0=ALU.mult,
                 )
-                att_words = att[:].bitcast(F32)
-                turned = psum_turn.tile([P, PASSES, 2, P], F32, name="turned")
+            for i in range(2):
+                att_words = att[i][:].bitcast(F32)
+                turned[r, i] = psum_turn.tile([P, PASSES, 2, P], F32, name="turned")
                 for g in range(PASSES):
                     for u in range(2):
                         first = (2 * g + u) * P
-                        nc.tensor.transpose(turned[:, g, u, :], att_words[:, first : first + P], ident[:])
-                nc.scalar.copy(out=grouped_words[:, i], in_=turned[:].rearrange("p g u c -> p g c u"))
+                        nc.tensor.transpose(turned[r, i][:, g, u, :], att_words[:, first : first + P], ident[:])
+
+        def quantise_att(r):
+            att_grouped = work.tile([P, 2 * C], BF16, name="att_grouped", align_bytes=64)
+            grouped_words = att_grouped[:].bitcast(F32).rearrange(
+                "p (i g c u) -> p i g c u", i=2, g=PASSES, u=2
+            )
+            for i in range(2):
+                nc.scalar.copy(out=grouped_words[:, i], in_=turned[r, i][:].rearrange("p g u c -> p g c u"))
             att_codes[r] = keep.tile([P, 2 * PASSES * P], U32, name="att_codes%d" % r, align_bytes=64)
             att_scales[r] = keep.tile([P, 2 * PASSES * P], U8, name="att_scales%d" % r, align_bytes=64)
+            return att_grouped
+
+        def quantise_att_end(r, att_grouped):
             nc.vector.quantize_mx(
                 out=att_codes[r][:].bitcast(FP8X4), scales=att_scales[r][:], in_=att_grouped[:]
             )
 
         xf_sb = []
         xl_sb = []
+        mean = {}
+        o_acc = {}
 
         def load_frames():
             for a in range(ROW_TILES // PACK):
@@ -217,11 +238,11 @@ def tile_coatten2_pb_kernel(tc, score_f, score_l, x_m, Wv, bv, gamma, x_f, x_l, 
                     nc.sync.dma_start(out=xf_sb[a][:, b, :], in_=x_f[rows, :])
                     nc.sync.dma_start(out=xl_sb[a][:, b, :], in_=x_l[rows, :])
 
-        def stage_two(r):
-            mean = work.tile([P, N], F32, name="mean")
+        def mean_of_frames(r):
+            mean[r] = long_work.tile([P, N], F32, name="mean")
             for h in range(HALVES):
                 cols = slice(h * HALF, (h + 1) * HALF)
-                mean_acc = psum_two.tile([P, HALF], F32, name="mean_acc", tag="two")
+                mean_acc = psum_mean.tile([P, HALF], F32, name="mean_acc")
                 nc.tensor.matmul(
                     out=mean_acc[:], lhsT=half_ident[:], rhs=xl_sb[r // PACK][:, r % PACK, cols],
                     start=True, stop=False,
@@ -230,15 +251,17 @@ def tile_coatten2_pb_kernel(tc, score_f, score_l, x_m, Wv, bv, gamma, x_f, x_l, 
                     out=mean_acc[:], lhsT=half_ident[:], rhs=xf_sb[r // PACK][:, r % PACK, cols],
                     start=False, stop=True,
                 )
-                nc.scalar.copy(out=mean[:, cols], in_=mean_acc[:])
+                nc.scalar.copy(out=mean[r][:, cols], in_=mean_acc[:])
+
+        def stage_two(r):
             for h in range(HALVES):
                 cols = slice(h * HALF, (h + 1) * HALF)
-                o_acc = psum_two.tile([P, HALF], F32, name="o_acc", tag="two")
+                o_acc[r, h] = psum_acc.tile([P, HALF], F32, name="o_acc", tag="acc")
                 for i in range(2):
                     for g in range(PASSES):
                         block = slice((i * PASSES + g) * P, (i * PASSES + g + 1) * P)
                         nc.tensor.matmul_mx(
-                            out=o_acc[:],
+                            out=o_acc[r, h][:],
                             lhsT=att_codes[r][:, block].bitcast(FP8X4),
                             lhsT_scale=att_scales[r][:, block],
                             rhs=v_codes[:, g, cols].bitcast(FP8X4),
@@ -246,12 +269,15 @@ def tile_coatten2_pb_kernel(tc, score_f, score_l, x_m, Wv, bv, gamma, x_f, x_l, 
                             start=(i == 0 and g == 0),
                             stop=(i == 1 and g == PASSES - 1),
                         )
-                result = work.tile([P, HALF], F32, name="result")
-                nc.vector.scalar_tensor_tensor(
-                    out=result[:], in0=o_acc[:], scalar=gain[:, 0:1], in1=mean[:, cols],
-                    op0=ALU.mult, op1=ALU.add,
-                )
-                nc.sync.dma_start(out=out[r * P : (r + 1) * P, cols], in_=result[:])
+
+        def fuse_and_store(r, h):
+            cols = slice(h * HALF, (h + 1) * HALF)
+            result = work.tile([P, HALF], F32, name="result")
+            nc.vector.scalar_tensor_tensor(
+                out=result[:], in0=o_acc[r, h][:], scalar=gain[:, 0:1], in1=mean[r][:, cols],
+                op0=ALU.mult, op1=ALU.add,
+            )
+            nc.sync.dma_start(out=out[r * P : (r + 1) * P, cols], in_=result[:])
 
         prepare_wv(0)
         for h in range(HALVES):
@@ -262,8 +288,34 @@ def tile_coatten2_pb_kernel(tc, score_f, score_l, x_m, Wv, bv, gamma, x_f, x_l, 
             for s in range(PASSES):
                 stage_one(h, s)
         for r in range(AHEAD):
-            softmax_tile(r)
-        for r in range(ROW_TILES):
-            if r + AHEAD < ROW_TILES:
-                softmax_tile(r + AHEAD)
-            stage_two(r)
+            for i in range(2):
+                row_max(r, i)
+            exponentials(r)
+            scale_and_turn(r)
+        quantise_att_end(0, quantise_att(0))
+        for i in range(2):
+            row_max(AHEAD, i)
+        for r in range(AHEAD):
+            mean_of_frames(r)
+
+        def in_range(r):
+            return 0 <= r < ROW_TILES
+
+        with tc.manual_schedule():
+            for a in range(AHEAD, ROW_TILES + 3):
+                if in_range(a):
+                    exponentials(a)
+                if in_range(a - 2):
+                    stage_two(a - 2)
+                for i in range(2):
+                    if in_range(a + 1):
+                        row_max(a + 1, i)
+                    if in_range(a - 3):
+                        fuse_and_store(a - 3, i)
+                if in_range(a - 1):
+                    att_grouped = quantise_att(a - 1)
+                if in_range(a):
+                    mean_of_frames(a)
+                    scale_and_turn(a)
+                if in_range(a - 1):
+                    quantise_att_end(a - 1, att_grouped)

@@ -37,6 +37,10 @@ def tile_coatten2_pb_kernel(tc, score_f, score_l, x_m, Wv, bv, gamma, x_f, x_l, 
         psum_acc = ctx.enter_context(tc.psum_pool(name="psum_acc", bufs=4))
         psum_mean = ctx.enter_context(tc.psum_pool(name="psum_mean", bufs=2))
 
+        warm = const.tile([P, 1], F32, name="warm")
+        nc.vector.memset(warm[:], 0.0)
+        warm_out = const.tile([P, 1], F32, name="warm_out")
+        nc.scalar.activation(out=warm_out[:], in_=warm[:], func=ACT.Exp)
         ident = const.tile([P, P], F32, name="ident")
         make_identity(nc, ident[:])
         half_ident = const.tile([P, P], BF16, name="half_ident")
@@ -80,9 +84,11 @@ def tile_coatten2_pb_kernel(tc, score_f, score_l, x_m, Wv, bv, gamma, x_f, x_l, 
         wv_codes = {}
         wv_scales = {}
 
-        def prepare_wv(s):
-            wv_grouped = keep.tile([P, PASSES * K_PASS * PACK], BF16, name="wv_grouped%d" % s, align_bytes=64)
-            grouped_words = wv_grouped[:].bitcast(F32).rearrange("p (g d u) -> p g d u", g=PASSES, u=2)
+        wv_grouped = {}
+
+        def turn_wv(s):
+            wv_grouped[s] = keep.tile([P, PASSES * K_PASS * PACK], BF16, name="wv_grouped%d" % s, align_bytes=64)
+            grouped_words = wv_grouped[s][:].bitcast(F32).rearrange("p (g d u) -> p g d u", g=PASSES, u=2)
             wv_words = wv_raw[s][:].rearrange("p t k -> p (t k)").bitcast(F32)
             for t in range(PACK):
                 turned = psum_acc.tile([P, PASSES, 2, P], F32, name="wv_turned", tag="acc")
@@ -94,12 +100,14 @@ def tile_coatten2_pb_kernel(tc, score_f, score_l, x_m, Wv, bv, gamma, x_f, x_l, 
                     out=grouped_words[:, :, t * P : (t + 1) * P, :],
                     in_=turned[:].rearrange("p g u d -> p g d u"),
                 )
+
+        def quantise_wv(s):
             wv_codes[s] = keep.tile([P, PASSES, K_PASS], U32, name="wv_codes%d" % s, align_bytes=64)
             wv_scales[s] = keep.tile([P, PASSES, K_PASS], U8, name="wv_scales%d" % s, align_bytes=64)
             nc.vector.quantize_mx(
                 out=wv_codes[s][:].rearrange("p g d -> p (g d)").bitcast(FP8X4),
                 scales=wv_scales[s][:].rearrange("p g d -> p (g d)"),
-                in_=wv_grouped[:],
+                in_=wv_grouped[s][:],
             )
 
         xm_codes = keep.tile([P, PASSES, N], U32, name="xm_codes", align_bytes=64)
@@ -111,25 +119,29 @@ def tile_coatten2_pb_kernel(tc, score_f, score_l, x_m, Wv, bv, gamma, x_f, x_l, 
                 in_=src.rearrange("p t (c i) -> p c t i", i=4),
             )
 
-        def prepare_xm(h):
+        xm_grouped = {}
+
+        def regroup_xm(g, h):
+            xm_grouped[g, h] = work.tile([P, HALF, PACK], BF16, name="xm_grouped", align_bytes=64)
+            regroup(xm_grouped[g, h][:], xm_raw[g][:, :, h * HALF : (h + 1) * HALF])
+
+        def quantise_xm(g, h):
             cols = slice(h * HALF, (h + 1) * HALF)
-            grouped = []
-            for g in range(PASSES):
-                grouped.append(work.tile([P, HALF, PACK], BF16, name="xm_grouped", align_bytes=64))
-                regroup(grouped[g][:], xm_raw[g][:, :, cols])
-            for g in range(PASSES):
-                nc.vector.quantize_mx(
-                    out=xm_codes[:, g, cols].bitcast(FP8X4),
-                    scales=xm_scales[:, g, cols],
-                    in_=grouped[g][:].rearrange("p n t -> p (n t)"),
-                )
+            nc.vector.quantize_mx(
+                out=xm_codes[:, g, cols].bitcast(FP8X4),
+                scales=xm_scales[:, g, cols],
+                in_=xm_grouped[g, h][:].rearrange("p n t -> p (n t)"),
+            )
 
         v_codes = keep.tile([P, PASSES, N], U32, name="v_codes", align_bytes=64)
         v_scales = keep.tile([P, PASSES, N], U8, name="v_scales", align_bytes=64)
 
+        v_rows = {}
+        v_grouped = {}
+
         def stage_one(h, s):
             cols = slice(h * HALF, (h + 1) * HALF)
-            v_rows = work.tile([P, PACK, HALF], BF16, name="v_rows")
+            v_rows[h, s] = long_work.tile([P, PACK, HALF], BF16, name="v_rows")
             for t in range(PACK):
                 v_acc = psum_acc.tile([P, HALF], F32, name="v_acc", tag="acc")
                 for g in range(PASSES):
@@ -143,18 +155,23 @@ def tile_coatten2_pb_kernel(tc, score_f, score_l, x_m, Wv, bv, gamma, x_f, x_l, 
                         stop=(g == PASSES - 1),
                     )
                 nc.scalar.activation(
-                    out=v_rows[:, t, :],
+                    out=v_rows[h, s][:, t, :],
                     in_=v_acc[:],
                     func=ACT.Identity,
                     bias=bias[:, s * PACK + t : s * PACK + t + 1],
                     scale=1.0,
                 )
-            v_grouped = work.tile([P, HALF, PACK], BF16, name="v_grouped", align_bytes=64)
-            regroup(v_grouped[:], v_rows[:])
+
+        def regroup_v(h, s):
+            v_grouped[h, s] = work.tile([P, HALF, PACK], BF16, name="v_grouped", align_bytes=64)
+            regroup(v_grouped[h, s][:], v_rows[h, s][:])
+
+        def quantise_v(h, s):
+            cols = slice(h * HALF, (h + 1) * HALF)
             nc.vector.quantize_mx(
                 out=v_codes[:, s, cols].bitcast(FP8X4),
                 scales=v_scales[:, s, cols],
-                in_=v_grouped[:].rearrange("p n t -> p (n t)"),
+                in_=v_grouped[h, s][:].rearrange("p n t -> p (n t)"),
             )
 
         neg_max = const.tile([P, 2 * ROW_TILES], F32, name="neg_max")
@@ -190,18 +207,23 @@ def tile_coatten2_pb_kernel(tc, score_f, score_l, x_m, Wv, bv, gamma, x_f, x_l, 
                     accum_out=row_sum[:, col],
                 )
 
-        def scale_and_turn(r):
+        att = {}
+
+        def reciprocals(r):
             both = slice(2 * r, 2 * r + 2)
             nc.vector.reciprocal(out=inv_sum[:, both], in_=row_sum[:, both])
-            att = []
+
+        def scale(r):
             for i in range(2):
-                att.append(work.tile([P, C], BF16, name="att"))
+                att[r, i] = work.tile([P, C], BF16, name="att")
                 nc.vector.tensor_scalar(
-                    out=att[i][:], in0=expo[r, i][:], scalar1=inv_sum[:, 2 * r + i : 2 * r + i + 1],
+                    out=att[r, i][:], in0=expo[r, i][:], scalar1=inv_sum[:, 2 * r + i : 2 * r + i + 1],
                     scalar2=None, op0=ALU.mult,
                 )
+
+        def turn(r):
             for i in range(2):
-                att_words = att[i][:].bitcast(F32)
+                att_words = att[r, i][:].bitcast(F32)
                 turned[r, i] = psum_turn.tile([P, PASSES, 2, P], F32, name="turned")
                 for g in range(PASSES):
                     for u in range(2):
@@ -272,36 +294,56 @@ def tile_coatten2_pb_kernel(tc, score_f, score_l, x_m, Wv, bv, gamma, x_f, x_l, 
 
         def fuse_and_store(r, h):
             cols = slice(h * HALF, (h + 1) * HALF)
-            result = work.tile([P, HALF], F32, name="result")
+            result = long_work.tile([P, HALF], F32, name="result")
             nc.vector.scalar_tensor_tensor(
                 out=result[:], in0=o_acc[r, h][:], scalar=gain[:, 0:1], in1=mean[r][:, cols],
                 op0=ALU.mult, op1=ALU.add,
             )
             nc.sync.dma_start(out=out[r * P : (r + 1) * P, cols], in_=result[:])
 
-        prepare_wv(0)
-        for h in range(HALVES):
-            prepare_xm(h)
-        prepare_wv(1)
-        load_frames()
-        for h in range(HALVES):
-            for s in range(PASSES):
-                stage_one(h, s)
-        for r in range(AHEAD):
-            for i in range(2):
-                row_max(r, i)
-            exponentials(r)
-            scale_and_turn(r)
-        quantise_att_end(0, quantise_att(0))
-        for i in range(2):
-            row_max(AHEAD, i)
-        for r in range(AHEAD):
-            mean_of_frames(r)
-
         def in_range(r):
             return 0 <= r < ROW_TILES
 
         with tc.manual_schedule():
+            for r in range(AHEAD):
+                for i in range(2):
+                    row_max(r, i)
+                exponentials(r)
+                if r == 0:
+                    turn_wv(0)
+            reciprocals(0)
+            scale(0)
+            turn(0)
+            quantise_wv(0)
+            for h in range(HALVES):
+                for g in range(PASSES):
+                    regroup_xm(g, h)
+                if h == 0:
+                    att_grouped = quantise_att(0)
+                    turn_wv(1)
+                for g in range(PASSES):
+                    quantise_xm(g, h)
+            load_frames()
+            for h in range(HALVES):
+                stage_one(h, 0)
+            reciprocals(1)
+            quantise_wv(1)
+            scale(1)
+            for h in range(HALVES):
+                stage_one(h, 1)
+            for i in range(2):
+                row_max(AHEAD, i)
+            pieces = [(h, s) for s in range(PASSES) for h in range(HALVES)]
+            regroup_v(*pieces[0])
+            for k in range(1, len(pieces)):
+                regroup_v(*pieces[k])
+                quantise_v(*pieces[k - 1])
+            quantise_att_end(0, att_grouped)
+            quantise_v(*pieces[-1])
+            for r in range(AHEAD):
+                mean_of_frames(r)
+            turn(1)
+
             for a in range(AHEAD, ROW_TILES + 3):
                 if in_range(a):
                     exponentials(a)
@@ -316,6 +358,8 @@ def tile_coatten2_pb_kernel(tc, score_f, score_l, x_m, Wv, bv, gamma, x_f, x_l, 
                     att_grouped = quantise_att(a - 1)
                 if in_range(a):
                     mean_of_frames(a)
-                    scale_and_turn(a)
+                    reciprocals(a)
+                    scale(a)
+                    turn(a)
                 if in_range(a - 1):
                     quantise_att_end(a - 1, att_grouped)

@@ -20,7 +20,8 @@ PASSES = C // K_PASS
 ROW_TILES = C // P
 HALF = 512
 HALVES = N // HALF
-AHEAD = 2
+MAPS = 2
+FIRST = 2
 
 FLOPS = 3 * 2 * C * C * N
 
@@ -34,13 +35,14 @@ def tile_coatten2_pb_kernel(tc, score_f, score_l, x_m, Wv, bv, gamma, x_f, x_l, 
         work = ctx.enter_context(tc.tile_pool(name="work", bufs=3))
         long_work = ctx.enter_context(tc.tile_pool(name="long_work", bufs=4))
         psum_turn = ctx.enter_context(tc.psum_pool(name="psum_turn", bufs=2))
-        psum_acc = ctx.enter_context(tc.psum_pool(name="psum_acc", bufs=4))
         psum_mean = ctx.enter_context(tc.psum_pool(name="psum_mean", bufs=2))
+        psum_acc = ctx.enter_context(tc.psum_pool(name="psum_acc", bufs=4))
 
         warm = const.tile([P, 1], F32, name="warm")
         nc.vector.memset(warm[:], 0.0)
         warm_out = const.tile([P, 1], F32, name="warm_out")
         nc.scalar.activation(out=warm_out[:], in_=warm[:], func=ACT.Exp)
+
         ident = const.tile([P, P], F32, name="ident")
         make_identity(nc, ident[:])
         half_ident = const.tile([P, P], BF16, name="half_ident")
@@ -56,13 +58,13 @@ def tile_coatten2_pb_kernel(tc, score_f, score_l, x_m, Wv, bv, gamma, x_f, x_l, 
         gain = const.tile([P, 1], F32, name="gain")
         nc.vector.tensor_copy(out=gain[:], in_=gain_bf[:])
 
-        scores = {"f": score_f, "l": score_l}
+        scores = (score_f, score_l)
         score_sb = {}
 
         def load_scores(r):
-            for x in ("f", "l"):
-                score_sb[x, r] = keep.tile([P, C], BF16, name="score_%s%d" % (x, r))
-                nc.sync.dma_start(out=score_sb[x, r][:], in_=scores[x][r * P : (r + 1) * P, :])
+            for i in range(MAPS):
+                score_sb[r, i] = keep.tile([P, C], BF16, name="score_%d_%d" % (r, i))
+                nc.sync.dma_start(out=score_sb[r, i][:], in_=scores[i][r * P : (r + 1) * P, :])
 
         def load_paired_rows(src, g, name):
             t = big.tile([P, PACK, src.shape[1]], BF16, name="%s%d" % (name, g), tag="big")
@@ -73,18 +75,29 @@ def tile_coatten2_pb_kernel(tc, score_f, score_l, x_m, Wv, bv, gamma, x_f, x_l, 
                 )
             return t
 
-        for r in range(AHEAD):
+        for r in range(FIRST):
             load_scores(r)
         wv_raw = [load_paired_rows(Wv, 0, "wv_raw")]
         xm_raw = [load_paired_rows(x_m, g, "xm_raw") for g in range(PASSES)]
         wv_raw.append(load_paired_rows(Wv, 1, "wv_raw"))
-        for r in range(AHEAD, ROW_TILES):
+        for r in range(FIRST, ROW_TILES):
             load_scores(r)
 
-        wv_codes = {}
-        wv_scales = {}
+        xf_sb = []
+        xl_sb = []
+
+        def load_frames():
+            for a in range(ROW_TILES // PACK):
+                xf_sb.append(big.tile([P, PACK, N], BF16, name="xf_sb%d" % a, tag="big"))
+                xl_sb.append(big.tile([P, PACK, N], BF16, name="xl_sb%d" % a, tag="big"))
+                for b in range(PACK):
+                    rows = slice((a * PACK + b) * P, (a * PACK + b + 1) * P)
+                    nc.sync.dma_start(out=xf_sb[a][:, b, :], in_=x_f[rows, :])
+                    nc.sync.dma_start(out=xl_sb[a][:, b, :], in_=x_l[rows, :])
 
         wv_grouped = {}
+        wv_codes = {}
+        wv_scales = {}
 
         def turn_wv(s):
             wv_grouped[s] = keep.tile([P, PASSES * K_PASS * PACK], BF16, name="wv_grouped%d" % s, align_bytes=64)
@@ -110,6 +123,7 @@ def tile_coatten2_pb_kernel(tc, score_f, score_l, x_m, Wv, bv, gamma, x_f, x_l, 
                 in_=wv_grouped[s][:],
             )
 
+        xm_grouped = {}
         xm_codes = keep.tile([P, PASSES, N], U32, name="xm_codes", align_bytes=64)
         xm_scales = keep.tile([P, PASSES, N], U8, name="xm_scales", align_bytes=64)
 
@@ -118,8 +132,6 @@ def tile_coatten2_pb_kernel(tc, score_f, score_l, x_m, Wv, bv, gamma, x_f, x_l, 
                 out=dst.rearrange("p (c i) t -> p c t i", i=4),
                 in_=src.rearrange("p t (c i) -> p c t i", i=4),
             )
-
-        xm_grouped = {}
 
         def regroup_xm(g, h):
             xm_grouped[g, h] = work.tile([P, HALF, PACK], BF16, name="xm_grouped", align_bytes=64)
@@ -133,11 +145,10 @@ def tile_coatten2_pb_kernel(tc, score_f, score_l, x_m, Wv, bv, gamma, x_f, x_l, 
                 in_=xm_grouped[g, h][:].rearrange("p n t -> p (n t)"),
             )
 
-        v_codes = keep.tile([P, PASSES, N], U32, name="v_codes", align_bytes=64)
-        v_scales = keep.tile([P, PASSES, N], U8, name="v_scales", align_bytes=64)
-
         v_rows = {}
         v_grouped = {}
+        v_codes = keep.tile([P, PASSES, N], U32, name="v_codes", align_bytes=64)
+        v_scales = keep.tile([P, PASSES, N], U8, name="v_scales", align_bytes=64)
 
         def stage_one(h, s):
             cols = slice(h * HALF, (h + 1) * HALF)
@@ -174,12 +185,13 @@ def tile_coatten2_pb_kernel(tc, score_f, score_l, x_m, Wv, bv, gamma, x_f, x_l, 
                 in_=v_grouped[h, s][:].rearrange("p n t -> p (n t)"),
             )
 
-        neg_max = const.tile([P, 2 * ROW_TILES], F32, name="neg_max")
-        row_sum = const.tile([P, 2 * ROW_TILES], F32, name="row_sum")
-        inv_sum = const.tile([P, 2 * ROW_TILES], F32, name="inv_sum")
-        maps = ("f", "l")
+        neg_max = const.tile([P, MAPS * ROW_TILES], F32, name="neg_max")
+        row_sum = const.tile([P, MAPS * ROW_TILES], F32, name="row_sum")
+        inv_sum = const.tile([P, MAPS * ROW_TILES], F32, name="inv_sum")
         expo = {}
-        turned = {}
+        att = {}
+        turned_att = {}
+        att_grouped = {}
         att_codes = {}
         att_scales = {}
 
@@ -187,99 +199,93 @@ def tile_coatten2_pb_kernel(tc, score_f, score_l, x_m, Wv, bv, gamma, x_f, x_l, 
             expo[r, i] = long_work.tile([P, C], F32, name="expo")
             nc.vector.tensor_scalar(
                 out=expo[r, i][:, 0 : C // 2].bitcast(BF16),
-                in0=score_sb[maps[i], r][:],
+                in0=score_sb[r, i][:],
                 scalar1=-1.0,
                 scalar2=None,
                 op0=ALU.mult,
                 op1=ALU.min,
-                accum_out=neg_max[:, 2 * r + i : 2 * r + i + 1],
+                accum_out=neg_max[:, MAPS * r + i : MAPS * r + i + 1],
             )
 
         def exponentials(r):
-            for i in range(2):
-                col = slice(2 * r + i, 2 * r + i + 1)
+            for i in range(MAPS):
+                col = slice(MAPS * r + i, MAPS * r + i + 1)
                 nc.scalar.activation(
                     out=expo[r, i][:],
-                    in_=score_sb[maps[i], r][:],
+                    in_=score_sb[r, i][:],
                     func=ACT.Exp,
                     bias=neg_max[:, col],
                     scale=1.0,
                     accum_out=row_sum[:, col],
                 )
 
-        att = {}
-
-        def reciprocals(r):
-            both = slice(2 * r, 2 * r + 2)
-            nc.vector.reciprocal(out=inv_sum[:, both], in_=row_sum[:, both])
+        def reciprocal(r, i):
+            col = slice(MAPS * r + i, MAPS * r + i + 1)
+            nc.vector.reciprocal(out=inv_sum[:, col], in_=row_sum[:, col])
 
         def scale(r):
-            for i in range(2):
+            for i in range(MAPS):
                 att[r, i] = work.tile([P, C], BF16, name="att")
                 nc.vector.tensor_scalar(
-                    out=att[r, i][:], in0=expo[r, i][:], scalar1=inv_sum[:, 2 * r + i : 2 * r + i + 1],
-                    scalar2=None, op0=ALU.mult,
+                    out=att[r, i][:], in0=expo[r, i][:],
+                    scalar1=inv_sum[:, MAPS * r + i : MAPS * r + i + 1], scalar2=None, op0=ALU.mult,
                 )
 
         def turn(r):
-            for i in range(2):
+            for i in range(MAPS):
                 att_words = att[r, i][:].bitcast(F32)
-                turned[r, i] = psum_turn.tile([P, PASSES, 2, P], F32, name="turned")
+                turned_att[r, i] = psum_turn.tile([P, PASSES, 2, P], F32, name="turned")
                 for g in range(PASSES):
                     for u in range(2):
                         first = (2 * g + u) * P
-                        nc.tensor.transpose(turned[r, i][:, g, u, :], att_words[:, first : first + P], ident[:])
+                        nc.tensor.transpose(
+                            turned_att[r, i][:, g, u, :], att_words[:, first : first + P], ident[:]
+                        )
+
+        def copy_att(r):
+            att_grouped[r] = work.tile([P, MAPS * C], BF16, name="att_grouped", align_bytes=64)
+            grouped_words = att_grouped[r][:].bitcast(F32).rearrange(
+                "p (i g c u) -> p i g c u", i=MAPS, g=PASSES, u=2
+            )
+            for i in range(MAPS):
+                nc.scalar.copy(
+                    out=grouped_words[:, i], in_=turned_att[r, i][:].rearrange("p g u c -> p g c u")
+                )
 
         def quantise_att(r):
-            att_grouped = work.tile([P, 2 * C], BF16, name="att_grouped", align_bytes=64)
-            grouped_words = att_grouped[:].bitcast(F32).rearrange(
-                "p (i g c u) -> p i g c u", i=2, g=PASSES, u=2
-            )
-            for i in range(2):
-                nc.scalar.copy(out=grouped_words[:, i], in_=turned[r, i][:].rearrange("p g u c -> p g c u"))
-            att_codes[r] = keep.tile([P, 2 * PASSES * P], U32, name="att_codes%d" % r, align_bytes=64)
-            att_scales[r] = keep.tile([P, 2 * PASSES * P], U8, name="att_scales%d" % r, align_bytes=64)
-            return att_grouped
-
-        def quantise_att_end(r, att_grouped):
+            att_codes[r] = keep.tile([P, MAPS * PASSES * P], U32, name="att_codes%d" % r, align_bytes=64)
+            att_scales[r] = keep.tile([P, MAPS * PASSES * P], U8, name="att_scales%d" % r, align_bytes=64)
             nc.vector.quantize_mx(
-                out=att_codes[r][:].bitcast(FP8X4), scales=att_scales[r][:], in_=att_grouped[:]
+                out=att_codes[r][:].bitcast(FP8X4), scales=att_scales[r][:], in_=att_grouped[r][:]
             )
 
-        xf_sb = []
-        xl_sb = []
+        mean_acc = {}
         mean = {}
         o_acc = {}
 
-        def load_frames():
-            for a in range(ROW_TILES // PACK):
-                xf_sb.append(big.tile([P, PACK, N], BF16, name="xf_sb%d" % a, tag="big"))
-                xl_sb.append(big.tile([P, PACK, N], BF16, name="xl_sb%d" % a, tag="big"))
-                for b in range(PACK):
-                    rows = slice((a * PACK + b) * P, (a * PACK + b + 1) * P)
-                    nc.sync.dma_start(out=xf_sb[a][:, b, :], in_=x_f[rows, :])
-                    nc.sync.dma_start(out=xl_sb[a][:, b, :], in_=x_l[rows, :])
-
-        def mean_of_frames(r):
-            mean[r] = long_work.tile([P, N], F32, name="mean")
+        def add_frames(r):
             for h in range(HALVES):
                 cols = slice(h * HALF, (h + 1) * HALF)
-                mean_acc = psum_mean.tile([P, HALF], F32, name="mean_acc")
+                mean_acc[r, h] = psum_mean.tile([P, HALF], F32, name="mean_acc")
                 nc.tensor.matmul(
-                    out=mean_acc[:], lhsT=half_ident[:], rhs=xl_sb[r // PACK][:, r % PACK, cols],
+                    out=mean_acc[r, h][:], lhsT=half_ident[:], rhs=xl_sb[r // PACK][:, r % PACK, cols],
                     start=True, stop=False,
                 )
                 nc.tensor.matmul(
-                    out=mean_acc[:], lhsT=half_ident[:], rhs=xf_sb[r // PACK][:, r % PACK, cols],
+                    out=mean_acc[r, h][:], lhsT=half_ident[:], rhs=xf_sb[r // PACK][:, r % PACK, cols],
                     start=False, stop=True,
                 )
-                nc.scalar.copy(out=mean[r][:, cols], in_=mean_acc[:])
+
+        def copy_mean(r):
+            mean[r] = work.tile([P, N], F32, name="mean")
+            for h in range(HALVES):
+                nc.scalar.copy(out=mean[r][:, h * HALF : (h + 1) * HALF], in_=mean_acc[r, h][:])
 
         def stage_two(r):
             for h in range(HALVES):
                 cols = slice(h * HALF, (h + 1) * HALF)
                 o_acc[r, h] = psum_acc.tile([P, HALF], F32, name="o_acc", tag="acc")
-                for i in range(2):
+                for i in range(MAPS):
                     for g in range(PASSES):
                         block = slice((i * PASSES + g) * P, (i * PASSES + g + 1) * P)
                         nc.tensor.matmul_mx(
@@ -289,7 +295,7 @@ def tile_coatten2_pb_kernel(tc, score_f, score_l, x_m, Wv, bv, gamma, x_f, x_l, 
                             rhs=v_codes[:, g, cols].bitcast(FP8X4),
                             rhs_scale=v_scales[:, g, cols],
                             start=(i == 0 and g == 0),
-                            stop=(i == 1 and g == PASSES - 1),
+                            stop=(i == MAPS - 1 and g == PASSES - 1),
                         )
 
         def fuse_and_store(r, h):
@@ -301,65 +307,80 @@ def tile_coatten2_pb_kernel(tc, score_f, score_l, x_m, Wv, bv, gamma, x_f, x_l, 
             )
             nc.sync.dma_start(out=out[r * P : (r + 1) * P, cols], in_=result[:])
 
-        def in_range(r):
-            return 0 <= r < ROW_TILES
-
         with tc.manual_schedule():
-            for r in range(AHEAD):
-                for i in range(2):
-                    row_max(r, i)
-                exponentials(r)
-                if r == 0:
-                    turn_wv(0)
-            reciprocals(0)
+            row_max(0, 0)
+            row_max(0, 1)
+            exponentials(0)
+            turn_wv(0)
+            row_max(1, 0)
+            row_max(1, 1)
+            exponentials(1)
+            reciprocal(0, 0)
+            reciprocal(0, 1)
             scale(0)
             turn(0)
             quantise_wv(0)
-            for h in range(HALVES):
-                for g in range(PASSES):
-                    regroup_xm(g, h)
-                if h == 0:
-                    att_grouped = quantise_att(0)
-                    turn_wv(1)
-                for g in range(PASSES):
-                    quantise_xm(g, h)
+            regroup_xm(0, 0)
+            regroup_xm(1, 0)
+            copy_att(0)
+            turn_wv(1)
+            quantise_xm(0, 0)
+            quantise_xm(1, 0)
+            regroup_xm(0, 1)
+            regroup_xm(1, 1)
+            quantise_xm(0, 1)
+            quantise_xm(1, 1)
             load_frames()
-            for h in range(HALVES):
-                stage_one(h, 0)
-            reciprocals(1)
+            stage_one(0, 0)
+            stage_one(1, 0)
+            reciprocal(1, 0)
+            reciprocal(1, 1)
             quantise_wv(1)
             scale(1)
-            for h in range(HALVES):
-                stage_one(h, 1)
-            for i in range(2):
-                row_max(AHEAD, i)
-            pieces = [(h, s) for s in range(PASSES) for h in range(HALVES)]
-            regroup_v(*pieces[0])
-            for k in range(1, len(pieces)):
-                regroup_v(*pieces[k])
-                quantise_v(*pieces[k - 1])
-            quantise_att_end(0, att_grouped)
-            quantise_v(*pieces[-1])
-            for r in range(AHEAD):
-                mean_of_frames(r)
+            stage_one(0, 1)
+            stage_one(1, 1)
+            row_max(FIRST, 0)
+            row_max(FIRST, 1)
+            regroup_v(0, 0)
+            regroup_v(1, 0)
+            quantise_v(0, 0)
+            regroup_v(0, 1)
+            quantise_v(1, 0)
+            regroup_v(1, 1)
+            quantise_v(0, 1)
+            quantise_att(0)
+            quantise_v(1, 1)
+            add_frames(0)
+            copy_mean(0)
             turn(1)
 
-            for a in range(AHEAD, ROW_TILES + 3):
-                if in_range(a):
+            def exists(r):
+                return 0 <= r < ROW_TILES
+
+            for a in range(FIRST, ROW_TILES + 3):
+                if exists(a):
                     exponentials(a)
-                if in_range(a - 2):
+                if exists(a - 1):
+                    add_frames(a - 1)
+                if exists(a - 2):
                     stage_two(a - 2)
-                for i in range(2):
-                    if in_range(a + 1):
-                        row_max(a + 1, i)
-                    if in_range(a - 3):
-                        fuse_and_store(a - 3, i)
-                if in_range(a - 1):
-                    att_grouped = quantise_att(a - 1)
-                if in_range(a):
-                    mean_of_frames(a)
-                    reciprocals(a)
+                if exists(a + 1):
+                    row_max(a + 1, 0)
+                if exists(a - 3):
+                    fuse_and_store(a - 3, 0)
+                if exists(a + 1):
+                    row_max(a + 1, 1)
+                if exists(a):
+                    reciprocal(a, 0)
+                if exists(a - 3):
+                    fuse_and_store(a - 3, 1)
+                if exists(a - 1):
+                    copy_att(a - 1)
+                    copy_mean(a - 1)
+                if exists(a):
+                    reciprocal(a, 1)
                     scale(a)
+                if exists(a - 1):
+                    quantise_att(a - 1)
+                if exists(a):
                     turn(a)
-                if in_range(a - 1):
-                    quantise_att_end(a - 1, att_grouped)

@@ -281,10 +281,14 @@ def tile_coatten2_pb_kernel(tc, score_f, score_l, x_m, Wv, bv, gamma, x_f, x_l, 
             for h in range(HALVES):
                 nc.scalar.copy(out=mean[r][:, h * HALF : (h + 1) * HALF], in_=mean_acc[r, h][:])
 
+        def pieces(r):
+            if r < ROW_TILES - 1:
+                return [slice(0, HALF), slice(HALF, N)]
+            return [slice(0, HALF), slice(HALF, HALF + HALF // 2), slice(HALF + HALF // 2, N)]
+
         def stage_two(r):
-            for h in range(HALVES):
-                cols = slice(h * HALF, (h + 1) * HALF)
-                o_acc[r, h] = psum_acc.tile([P, HALF], F32, name="o_acc", tag="acc")
+            for h, cols in enumerate(pieces(r)):
+                o_acc[r, h] = psum_acc.tile([P, cols.stop - cols.start], F32, name="o_acc", tag="acc")
                 for i in range(MAPS):
                     for g in range(PASSES):
                         block = slice((i * PASSES + g) * P, (i * PASSES + g + 1) * P)
@@ -299,8 +303,8 @@ def tile_coatten2_pb_kernel(tc, score_f, score_l, x_m, Wv, bv, gamma, x_f, x_l, 
                         )
 
         def fuse_and_store(r, h):
-            cols = slice(h * HALF, (h + 1) * HALF)
-            result = long_work.tile([P, HALF], F32, name="result")
+            cols = pieces(r)[h]
+            result = long_work.tile([P, cols.stop - cols.start], F32, name="result")
             nc.vector.scalar_tensor_tensor(
                 out=result[:], in0=o_acc[r, h][:], scalar=gain[:, 0:1], in1=mean[r][:, cols],
                 op0=ALU.mult, op1=ALU.add,
@@ -373,7 +377,8 @@ def tile_coatten2_pb_kernel(tc, score_f, score_l, x_m, Wv, bv, gamma, x_f, x_l, 
                 if exists(a):
                     reciprocal(a, 0)
                 if exists(a - 3):
-                    fuse_and_store(a - 3, 1)
+                    for h in range(1, len(pieces(a - 3))):
+                        fuse_and_store(a - 3, h)
                 if exists(a - 1):
                     copy_att(a - 1)
                     copy_mean(a - 1)

@@ -50,13 +50,9 @@ def tile_coatten2_pb_kernel(tc, score_f, score_l, x_m, Wv, bv, gamma, x_f, x_l, 
             out=half_ident[:], in0=ident[:], scalar1=0.5, scalar2=None, op0=ALU.mult
         )
         bias_bf = const.tile([P, PASSES * 2, 2], BF16, name="bias_bf")
-        nc.scalar.dma_start(out=bias_bf[:], in_=bv.rearrange("(a p e) -> p a e", p=P, e=2))
         bias = const.tile([P, PASSES * PACK], F32, name="bias")
-        nc.vector.tensor_copy(out=bias[:], in_=bias_bf[:].rearrange("p a e -> p (a e)"))
         gain_bf = const.tile([P, 1], BF16, name="gain_bf")
-        nc.scalar.dma_start(out=gain_bf[:], in_=gamma.partition_broadcast(P))
         gain = const.tile([P, 1], F32, name="gain")
-        nc.vector.tensor_copy(out=gain[:], in_=gain_bf[:])
 
         scores = (score_f, score_l)
         score_sb = {}
@@ -80,6 +76,8 @@ def tile_coatten2_pb_kernel(tc, score_f, score_l, x_m, Wv, bv, gamma, x_f, x_l, 
         wv_raw = [load_paired_rows(Wv, 0, "wv_raw")]
         xm_raw = [load_paired_rows(x_m, g, "xm_raw") for g in range(PASSES)]
         wv_raw.append(load_paired_rows(Wv, 1, "wv_raw"))
+        nc.sync.dma_start(out=bias_bf[:], in_=bv.rearrange("(a p e) -> p a e", p=P, e=2))
+        nc.sync.dma_start(out=gain_bf[:], in_=gamma.partition_broadcast(P))
         for r in range(FIRST, ROW_TILES):
             load_scores(r)
 
@@ -332,6 +330,8 @@ def tile_coatten2_pb_kernel(tc, score_f, score_l, x_m, Wv, bv, gamma, x_f, x_l, 
             quantise_xm(1, 0)
             regroup_xm(0, 1)
             regroup_xm(1, 1)
+            nc.vector.tensor_copy(out=bias[:], in_=bias_bf[:].rearrange("p a e -> p (a e)"))
+            nc.vector.tensor_copy(out=gain[:], in_=gain_bf[:])
             quantise_xm(0, 1)
             quantise_xm(1, 1)
             load_frames()

@@ -21,6 +21,7 @@ ROW_TILES = C // P
 HALF = 512
 HALVES = N // HALF
 MAPS = 2
+LAST = ROW_TILES - 1
 FIRST = 2
 
 FLOPS = 3 * 2 * C * C * N
@@ -49,7 +50,8 @@ def tile_coatten2_pb_kernel(tc, score_f, score_l, x_m, Wv, bv, gamma, x_f, x_l, 
         nc.vector.tensor_scalar(
             out=half_ident[:], in0=ident[:], scalar1=0.5, scalar2=None, op0=ALU.mult
         )
-        bias_bf = const.tile([P, PASSES * 2, 2], BF16, name="bias_bf")
+        bias_rows = const.tile([P, 2 * P], BF16, name="bias_rows")
+        nc.gpsimd.memset(bias_rows[:], 0.0)
         bias = const.tile([P, PASSES * PACK], F32, name="bias")
         gain_bf = const.tile([P, 1], BF16, name="gain_bf")
         gain = const.tile([P, 1], F32, name="gain")
@@ -73,13 +75,15 @@ def tile_coatten2_pb_kernel(tc, score_f, score_l, x_m, Wv, bv, gamma, x_f, x_l, 
 
         for r in range(FIRST):
             load_scores(r)
+        nc.sync.dma_start(
+            out=bias_rows[0 : 2 * PASSES, :], in_=bv.rearrange("(a w) -> a w", a=2 * PASSES)
+        )
         wv_raw = [load_paired_rows(Wv, 0, "wv_raw")]
         xm_raw = [load_paired_rows(x_m, g, "xm_raw") for g in range(PASSES)]
         wv_raw.append(load_paired_rows(Wv, 1, "wv_raw"))
-        nc.sync.dma_start(out=bias_bf[:], in_=bv.rearrange("(a p e) -> p a e", p=P, e=2))
-        nc.sync.dma_start(out=gain_bf[:], in_=gamma.partition_broadcast(P))
         for r in range(FIRST, ROW_TILES):
             load_scores(r)
+        nc.sync.dma_start(out=gain_bf[:], in_=gamma.partition_broadcast(P))
 
         xf_sb = []
         xl_sb = []
@@ -92,6 +96,11 @@ def tile_coatten2_pb_kernel(tc, score_f, score_l, x_m, Wv, bv, gamma, x_f, x_l, 
                     rows = slice((a * PACK + b) * P, (a * PACK + b + 1) * P)
                     nc.sync.dma_start(out=xf_sb[a][:, b, :], in_=x_f[rows, :])
                     nc.sync.dma_start(out=xl_sb[a][:, b, :], in_=x_l[rows, :])
+
+        def turn_bias():
+            turned = psum_acc.tile([P, P], F32, name="bias_turned", tag="acc")
+            nc.tensor.transpose(turned[:], bias_rows[:].bitcast(F32), ident[:])
+            nc.scalar.copy(out=bias[:], in_=turned[:, 0 : 2 * PASSES].bitcast(BF16))
 
         wv_grouped = {}
         wv_codes = {}
@@ -221,8 +230,15 @@ def tile_coatten2_pb_kernel(tc, score_f, score_l, x_m, Wv, bv, gamma, x_f, x_l, 
             col = slice(MAPS * r + i, MAPS * r + i + 1)
             nc.vector.reciprocal(out=inv_sum[:, col], in_=row_sum[:, col])
 
-        def scale(r):
-            for i in range(MAPS):
+        def scale_by_scalar(r, i):
+            att[r, i] = work.tile([P, C], BF16, name="att")
+            nc.scalar.activation(
+                out=att[r, i][:], in_=expo[r, i][:], func=ACT.Copy,
+                scale=inv_sum[:, MAPS * r + i : MAPS * r + i + 1],
+            )
+
+        def scale(r, maps=range(MAPS)):
+            for i in maps:
                 att[r, i] = work.tile([P, C], BF16, name="att")
                 nc.vector.tensor_scalar(
                     out=att[r, i][:], in0=expo[r, i][:],
@@ -274,6 +290,17 @@ def tile_coatten2_pb_kernel(tc, score_f, score_l, x_m, Wv, bv, gamma, x_f, x_l, 
                     start=False, stop=True,
                 )
 
+        def vector_mean(r):
+            a, b = r // PACK, r % PACK
+            mean[r] = work.tile([P, N], F32, name="mean")
+            nc.vector.tensor_scalar(
+                out=xf_sb[a][:, b, :], in0=xf_sb[a][:, b, :], scalar1=0.5, scalar2=None, op0=ALU.mult
+            )
+            nc.vector.scalar_tensor_tensor(
+                out=mean[r][:], in0=xl_sb[a][:, b, :], scalar=0.5, in1=xf_sb[a][:, b, :],
+                op0=ALU.mult, op1=ALU.add,
+            )
+
         def copy_mean(r):
             mean[r] = work.tile([P, N], F32, name="mean")
             for h in range(HALVES):
@@ -313,6 +340,7 @@ def tile_coatten2_pb_kernel(tc, score_f, score_l, x_m, Wv, bv, gamma, x_f, x_l, 
             row_max(0, 0)
             row_max(0, 1)
             exponentials(0)
+            turn_bias()
             turn_wv(0)
             row_max(1, 0)
             row_max(1, 1)
@@ -323,24 +351,23 @@ def tile_coatten2_pb_kernel(tc, score_f, score_l, x_m, Wv, bv, gamma, x_f, x_l, 
             turn(0)
             quantise_wv(0)
             regroup_xm(0, 0)
+            reciprocal(1, 0)
+            reciprocal(1, 1)
             regroup_xm(1, 0)
             copy_att(0)
+            scale_by_scalar(1, 0)
             turn_wv(1)
             quantise_xm(0, 0)
             quantise_xm(1, 0)
             regroup_xm(0, 1)
             regroup_xm(1, 1)
-            nc.vector.tensor_copy(out=bias[:], in_=bias_bf[:].rearrange("p a e -> p (a e)"))
-            nc.vector.tensor_copy(out=gain[:], in_=gain_bf[:])
             quantise_xm(0, 1)
             quantise_xm(1, 1)
             load_frames()
             stage_one(0, 0)
             stage_one(1, 0)
-            reciprocal(1, 0)
-            reciprocal(1, 1)
             quantise_wv(1)
-            scale(1)
+            scale(1, (1,))
             stage_one(0, 1)
             stage_one(1, 1)
             row_max(FIRST, 0)
@@ -354,6 +381,7 @@ def tile_coatten2_pb_kernel(tc, score_f, score_l, x_m, Wv, bv, gamma, x_f, x_l, 
             quantise_v(0, 1)
             quantise_att(0)
             quantise_v(1, 1)
+            nc.gpsimd.tensor_copy(out=gain[:], in_=gain_bf[:])
             add_frames(0)
             copy_mean(0)
             turn(1)
@@ -364,7 +392,7 @@ def tile_coatten2_pb_kernel(tc, score_f, score_l, x_m, Wv, bv, gamma, x_f, x_l, 
             for a in range(FIRST, ROW_TILES + 3):
                 if exists(a):
                     exponentials(a)
-                if exists(a - 1):
+                if exists(a - 1) and a - 1 < LAST:
                     add_frames(a - 1)
                 if exists(a - 2):
                     stage_two(a - 2)
@@ -374,6 +402,8 @@ def tile_coatten2_pb_kernel(tc, score_f, score_l, x_m, Wv, bv, gamma, x_f, x_l, 
                     fuse_and_store(a - 3, 0)
                 if exists(a + 1):
                     row_max(a + 1, 1)
+                if a == LAST:
+                    vector_mean(a)
                 if exists(a):
                     reciprocal(a, 0)
                 if exists(a - 3):
@@ -381,7 +411,8 @@ def tile_coatten2_pb_kernel(tc, score_f, score_l, x_m, Wv, bv, gamma, x_f, x_l, 
                         fuse_and_store(a - 3, h)
                 if exists(a - 1):
                     copy_att(a - 1)
-                    copy_mean(a - 1)
+                    if a - 1 < LAST:
+                        copy_mean(a - 1)
                 if exists(a):
                     reciprocal(a, 1)
                     scale(a)

@@ -50,10 +50,11 @@ def tile_coatten2_pb_kernel(tc, score_f, score_l, x_m, Wv, bv, gamma, x_f, x_l, 
         nc.vector.tensor_scalar(
             out=half_ident[:], in0=ident[:], scalar1=0.5, scalar2=None, op0=ALU.mult
         )
-        bias_rows = const.tile([P, 2 * P], BF16, name="bias_rows")
-        nc.gpsimd.memset(bias_rows[:], 0.0)
+        small_rows = const.tile([P, 2 * P + 2], BF16, name="small_rows")
+        nc.gpsimd.memset(small_rows[:], 0.0)
+        ones = const.tile([P, P], BF16, name="ones")
+        nc.gpsimd.memset(ones[:], 1.0)
         bias = const.tile([P, PASSES * PACK], F32, name="bias")
-        gain_bf = const.tile([P, 1], BF16, name="gain_bf")
         gain = const.tile([P, 1], F32, name="gain")
 
         scores = (score_f, score_l)
@@ -64,26 +65,33 @@ def tile_coatten2_pb_kernel(tc, score_f, score_l, x_m, Wv, bv, gamma, x_f, x_l, 
                 score_sb[r, i] = keep.tile([P, C], BF16, name="score_%d_%d" % (r, i))
                 nc.sync.dma_start(out=score_sb[r, i][:], in_=scores[i][r * P : (r + 1) * P, :])
 
-        def load_paired_rows(src, g, name):
-            t = big.tile([P, PACK, src.shape[1]], BF16, name="%s%d" % (name, g), tag="big")
-            for u in range(2):
+        def paired_tile(src, g, name):
+            return big.tile([P, PACK, src.shape[1]], BF16, name="%s%d" % (name, g), tag="big")
+
+        def load_paired_rows(t, src, g, pairs=range(2)):
+            for u in pairs:
                 rows = src[g * K_PASS + u * 2 * P : g * K_PASS + (u + 1) * 2 * P, :]
                 nc.sync.dma_start(
                     out=t[:, 2 * u : 2 * u + 2, :], in_=rows.rearrange("(p e) n -> p e n", e=2)
                 )
-            return t
 
         for r in range(FIRST):
             load_scores(r)
         nc.sync.dma_start(
-            out=bias_rows[0 : 2 * PASSES, :], in_=bv.rearrange("(a w) -> a w", a=2 * PASSES)
+            out=small_rows[0 : 2 * PASSES, 0 : 2 * P], in_=bv.rearrange("(a w) -> a w", a=2 * PASSES)
         )
-        wv_raw = [load_paired_rows(Wv, 0, "wv_raw")]
-        xm_raw = [load_paired_rows(x_m, g, "xm_raw") for g in range(PASSES)]
-        wv_raw.append(load_paired_rows(Wv, 1, "wv_raw"))
+        nc.sync.dma_start(
+            out=small_rows[0:1, 2 * P : 2 * P + 1], in_=gamma.rearrange("(a w) -> a w", a=1)
+        )
+        wv_raw = [paired_tile(Wv, s, "wv_raw") for s in range(PASSES)]
+        xm_raw = [paired_tile(x_m, g, "xm_raw") for g in range(PASSES)]
+        load_paired_rows(wv_raw[0], Wv, 0, (0,))
+        for g in range(PASSES):
+            load_paired_rows(xm_raw[g], x_m, g)
+        load_paired_rows(wv_raw[0], Wv, 0, (1,))
+        load_paired_rows(wv_raw[1], Wv, 1)
         for r in range(FIRST, ROW_TILES):
             load_scores(r)
-        nc.sync.dma_start(out=gain_bf[:], in_=gamma.partition_broadcast(P))
 
         xf_sb = []
         xl_sb = []
@@ -97,37 +105,44 @@ def tile_coatten2_pb_kernel(tc, score_f, score_l, x_m, Wv, bv, gamma, x_f, x_l, 
                     nc.sync.dma_start(out=xf_sb[a][:, b, :], in_=x_f[rows, :])
                     nc.sync.dma_start(out=xl_sb[a][:, b, :], in_=x_l[rows, :])
 
-        def turn_bias():
-            turned = psum_acc.tile([P, P], F32, name="bias_turned", tag="acc")
-            nc.tensor.transpose(turned[:], bias_rows[:].bitcast(F32), ident[:])
+        def spread_small():
+            turned = psum_acc.tile([P, P + 1], F32, name="small_turned", tag="acc")
+            nc.tensor.transpose(turned[:, 0:P], small_rows[:, 0 : 2 * P].bitcast(F32), ident[:])
+            nc.tensor.matmul(
+                out=turned[:, P : P + 1], lhsT=ones[:], rhs=small_rows[:, 2 * P : 2 * P + 1],
+                start=True, stop=True,
+            )
             nc.scalar.copy(out=bias[:], in_=turned[:, 0 : 2 * PASSES].bitcast(BF16))
+            nc.scalar.copy(out=gain[:], in_=turned[:, P : P + 1])
 
         wv_grouped = {}
         wv_codes = {}
         wv_scales = {}
 
-        def turn_wv(s):
-            wv_grouped[s] = keep.tile([P, PASSES * K_PASS * PACK], BF16, name="wv_grouped%d" % s, align_bytes=64)
-            grouped_words = wv_grouped[s][:].bitcast(F32).rearrange("p (g d u) -> p g d u", g=PASSES, u=2)
+        def turn_wv(s, rows=range(PACK), copy=nc.scalar.copy):
+            if s not in wv_grouped:
+                wv_grouped[s] = keep.tile([P, PACK * PASSES * P * PACK], BF16, name="wv_grouped%d" % s, align_bytes=64)
+                wv_codes[s] = keep.tile([P, PACK, PASSES, P], U32, name="wv_codes%d" % s, align_bytes=64)
+                wv_scales[s] = keep.tile([P, PACK, PASSES, P], U8, name="wv_scales%d" % s, align_bytes=64)
+            grouped_words = wv_grouped[s][:].bitcast(F32).rearrange(
+                "p (t g d u) -> p t g d u", t=PACK, g=PASSES, u=2
+            )
             wv_words = wv_raw[s][:].rearrange("p t k -> p (t k)").bitcast(F32)
-            for t in range(PACK):
+            for t in rows:
                 turned = psum_acc.tile([P, PASSES, 2, P], F32, name="wv_turned", tag="acc")
                 for g in range(PASSES):
                     for u in range(2):
                         first = t * (C // 2) + (2 * g + u) * P
                         nc.tensor.transpose(turned[:, g, u, :], wv_words[:, first : first + P], ident[:])
-                nc.scalar.copy(
-                    out=grouped_words[:, :, t * P : (t + 1) * P, :],
-                    in_=turned[:].rearrange("p g u d -> p g d u"),
-                )
+                copy(out=grouped_words[:, t], in_=turned[:].rearrange("p g u d -> p g d u"))
 
-        def quantise_wv(s):
-            wv_codes[s] = keep.tile([P, PASSES, K_PASS], U32, name="wv_codes%d" % s, align_bytes=64)
-            wv_scales[s] = keep.tile([P, PASSES, K_PASS], U8, name="wv_scales%d" % s, align_bytes=64)
+        def quantise_wv(s, first=0, count=PACK):
+            rows = slice(first, first + count)
+            values = PASSES * P * PACK
             nc.vector.quantize_mx(
-                out=wv_codes[s][:].rearrange("p g d -> p (g d)").bitcast(FP8X4),
-                scales=wv_scales[s][:].rearrange("p g d -> p (g d)"),
-                in_=wv_grouped[s][:],
+                out=wv_codes[s][:, rows].rearrange("p t g d -> p (t g d)").bitcast(FP8X4),
+                scales=wv_scales[s][:, rows].rearrange("p t g d -> p (t g d)"),
+                in_=wv_grouped[s][:, first * values : (first + count) * values],
             )
 
         xm_grouped = {}
@@ -165,8 +180,8 @@ def tile_coatten2_pb_kernel(tc, score_f, score_l, x_m, Wv, bv, gamma, x_f, x_l, 
                 for g in range(PASSES):
                     nc.tensor.matmul_mx(
                         out=v_acc[:],
-                        lhsT=wv_codes[s][:, g, t * P : (t + 1) * P].bitcast(FP8X4),
-                        lhsT_scale=wv_scales[s][:, g, t * P : (t + 1) * P],
+                        lhsT=wv_codes[s][:, t, g].bitcast(FP8X4),
+                        lhsT_scale=wv_scales[s][:, t, g],
                         rhs=xm_codes[:, g, cols].bitcast(FP8X4),
                         rhs_scale=xm_scales[:, g, cols],
                         start=(g == 0),
@@ -340,26 +355,28 @@ def tile_coatten2_pb_kernel(tc, score_f, score_l, x_m, Wv, bv, gamma, x_f, x_l, 
             row_max(0, 0)
             row_max(0, 1)
             exponentials(0)
-            turn_bias()
-            turn_wv(0)
+            spread_small()
+            turn_wv(0, (0, 1))
             row_max(1, 0)
             row_max(1, 1)
             exponentials(1)
             reciprocal(0, 0)
             reciprocal(0, 1)
             scale(0)
+            quantise_wv(0, 0, 2)
             turn(0)
-            quantise_wv(0)
             regroup_xm(0, 0)
             reciprocal(1, 0)
             reciprocal(1, 1)
             regroup_xm(1, 0)
             copy_att(0)
             scale_by_scalar(1, 0)
-            turn_wv(1)
+            turn_wv(0, (2, 3))
             quantise_xm(0, 0)
             quantise_xm(1, 0)
+            turn_wv(1)
             regroup_xm(0, 1)
+            quantise_wv(0, 2, 2)
             regroup_xm(1, 1)
             quantise_xm(0, 1)
             quantise_xm(1, 1)
@@ -381,7 +398,6 @@ def tile_coatten2_pb_kernel(tc, score_f, score_l, x_m, Wv, bv, gamma, x_f, x_l, 
             quantise_v(0, 1)
             quantise_att(0)
             quantise_v(1, 1)
-            nc.gpsimd.tensor_copy(out=gain[:], in_=gain_bf[:])
             add_frames(0)
             copy_mean(0)
             turn(1)

from contextlib import ExitStack

import concourse.mybir as mybir
from concourse.masks import make_identity

FP8X4 = mybir.dt.float8_e4m3fn_x4
BF16 = mybir.dt.bfloat16
F32 = mybir.dt.float32
U32 = mybir.dt.uint32
U8 = mybir.dt.uint8
ALU = mybir.AluOpType
ACT = mybir.ActivationFunctionType

P = 128
PACK = 4
K_PASS = P * PACK
C = 1024
N = 1024
PASSES = C // K_PASS
ROW_TILES = C // P
HALF = 512
HALVES = N // HALF
MAPS = 2
LAST = ROW_TILES - 1
FIRST = 2

FLOPS = 3 * 2 * C * C * N


def tile_coatten2_pb_kernel(tc, score_f, score_l, x_m, Wv, bv, gamma, x_f, x_l, out):
    nc = tc.nc
    with ExitStack() as ctx:
        const = ctx.enter_context(tc.tile_pool(name="const", bufs=1))
        keep = ctx.enter_context(tc.tile_pool(name="keep", bufs=1))
        big = ctx.enter_context(tc.tile_pool(name="big", bufs=4))
        work = ctx.enter_context(tc.tile_pool(name="work", bufs=3))
        long_work = ctx.enter_context(tc.tile_pool(name="long_work", bufs=4))
        psum_turn = ctx.enter_context(tc.psum_pool(name="psum_turn", bufs=2))
        psum_mean = ctx.enter_context(tc.psum_pool(name="psum_mean", bufs=2))
        psum_acc = ctx.enter_context(tc.psum_pool(name="psum_acc", bufs=4))

        warm = const.tile([P, 1], F32, name="warm")
        nc.vector.memset(warm[:], 0.0)
        warm_out = const.tile([P, 1], F32, name="warm_out")
        nc.scalar.activation(out=warm_out[:], in_=warm[:], func=ACT.Exp)

        ident = const.tile([P, P], F32, name="ident")
        make_identity(nc, ident[:])
        half_ident = const.tile([P, P], BF16, name="half_ident")
        nc.vector.tensor_scalar(
            out=half_ident[:], in0=ident[:], scalar1=0.5, scalar2=None, op0=ALU.mult
        )
        small_rows = const.tile([P, 2 * P + 2], BF16, name="small_rows")
        nc.gpsimd.memset(small_rows[:], 0.0)
        ones = const.tile([P, P], BF16, name="ones")
        nc.gpsimd.memset(ones[:], 1.0)
        bias = const.tile([P, PASSES * PACK], F32, name="bias")
        gain = const.tile([P, 1], F32, name="gain")

        scores = (score_f, score_l)
        score_sb = {}

        def load_scores(r):
            for i in range(MAPS):
                score_sb[r, i] = keep.tile([P, C], BF16, name="score_%d_%d" % (r, i))
                nc.sync.dma_start(out=score_sb[r, i][:], in_=scores[i][r * P : (r + 1) * P, :])

        def paired_tile(src, g, name):
            return big.tile([P, PACK, src.shape[1]], BF16, name="%s%d" % (name, g), tag="big")

        def load_paired_rows(t, src, g, pairs=range(2)):
            for u in pairs:
                rows = src[g * K_PASS + u * 2 * P : g * K_PASS + (u + 1) * 2 * P, :]
                nc.sync.dma_start(
                    out=t[:, 2 * u : 2 * u + 2, :], in_=rows.rearrange("(p e) n -> p e n", e=2)
                )

        for r in range(FIRST):
            load_scores(r)
        nc.sync.dma_start(
            out=small_rows[0 : 2 * PASSES, 0 : 2 * P], in_=bv.rearrange("(a w) -> a w", a=2 * PASSES)
        )
        nc.sync.dma_start(
            out=small_rows[0:1, 2 * P : 2 * P + 1], in_=gamma.rearrange("(a w) -> a w", a=1)
        )
        wv_raw = [paired_tile(Wv, s, "wv_raw") for s in range(PASSES)]
        xm_raw = [paired_tile(x_m, g, "xm_raw") for g in range(PASSES)]
        load_paired_rows(wv_raw[0], Wv, 0, (0,))
        for g in range(PASSES):
            load_paired_rows(xm_raw[g], x_m, g)
        load_paired_rows(wv_raw[0], Wv, 0, (1,))
        load_paired_rows(wv_raw[1], Wv, 1)
        for r in range(FIRST, ROW_TILES):
            load_scores(r)

        xf_sb = []
        xl_sb = []

        def load_frames():
            for a in range(ROW_TILES // PACK):
                xf_sb.append(big.tile([P, PACK, N], BF16, name="xf_sb%d" % a, tag="big"))
                xl_sb.append(big.tile([P, PACK, N], BF16, name="xl_sb%d" % a, tag="big"))
                for b in range(PACK):
                    rows = slice((a * PACK + b) * P, (a * PACK + b + 1) * P)
                    nc.sync.dma_start(out=xf_sb[a][:, b, :], in_=x_f[rows, :])
                    nc.sync.dma_start(out=xl_sb[a][:, b, :], in_=x_l[rows, :])

        def spread_small():
            turned = psum_acc.tile([P, P + 1], F32, name="small_turned", tag="acc")
            nc.tensor.transpose(turned[:, 0:P], small_rows[:, 0 : 2 * P].bitcast(F32), ident[:])
            nc.tensor.matmul(
                out=turned[:, P : P + 1], lhsT=ones[:], rhs=small_rows[:, 2 * P : 2 * P + 1],
                start=True, stop=True,
            )
            nc.scalar.copy(out=bias[:], in_=turned[:, 0 : 2 * PASSES].bitcast(BF16))
            nc.scalar.copy(out=gain[:], in_=turned[:, P : P + 1])

        wv_grouped = {}
        wv_codes = {}
        wv_scales = {}

        def turn_wv(s, rows=range(PACK), copy=nc.scalar.copy):
            if s not in wv_grouped:
                wv_grouped[s] = keep.tile([P, PACK * PASSES * P * PACK], BF16, name="wv_grouped%d" % s, align_bytes=64)
                wv_codes[s] = keep.tile([P, PACK, PASSES, P], U32, name="wv_codes%d" % s, align_bytes=64)
                wv_scales[s] = keep.tile([P, PACK, PASSES, P], U8, name="wv_scales%d" % s, align_bytes=64)
            grouped_words = wv_grouped[s][:].bitcast(F32).rearrange(
                "p (t g d u) -> p t g d u", t=PACK, g=PASSES, u=2
            )
            wv_words = wv_raw[s][:].rearrange("p t k -> p (t k)").bitcast(F32)
            for t in rows:
                turned = psum_acc.tile([P, PASSES, 2, P], F32, name="wv_turned", tag="acc")
                for g in range(PASSES):
                    for u in range(2):
                        first = t * (C // 2) + (2 * g + u) * P
                        nc.tensor.transpose(turned[:, g, u, :], wv_words[:, first : first + P], ident[:])
                copy(out=grouped_words[:, t], in_=turned[:].rearrange("p g u d -> p g d u"))

        def quantise_wv(s, first=0, count=PACK):
            rows = slice(first, first + count)
            values = PASSES * P * PACK
            nc.vector.quantize_mx(
                out=wv_codes[s][:, rows].rearrange("p t g d -> p (t g d)").bitcast(FP8X4),
                scales=wv_scales[s][:, rows].rearrange("p t g d -> p (t g d)"),
                in_=wv_grouped[s][:, first * values : (first + count) * values],
            )

        xm_grouped = {}
        xm_codes = keep.tile([P, PASSES, N], U32, name="xm_codes", align_bytes=64)
        xm_scales = keep.tile([P, PASSES, N], U8, name="xm_scales", align_bytes=64)

        def regroup(dst, src):
            nc.vector.tensor_copy(
                out=dst.rearrange("p (c i) t -> p c t i", i=4),
                in_=src.rearrange("p t (c i) -> p c t i", i=4),
            )

        def regroup_xm(g, h):
            xm_grouped[g, h] = work.tile([P, HALF, PACK], BF16, name="xm_grouped", align_bytes=64)
            regroup(xm_grouped[g, h][:], xm_raw[g][:, :, h * HALF : (h + 1) * HALF])

        def quantise_xm(g, h):
            cols = slice(h * HALF, (h + 1) * HALF)
            nc.vector.quantize_mx(
                out=xm_codes[:, g, cols].bitcast(FP8X4),
                scales=xm_scales[:, g, cols],
                in_=xm_grouped[g, h][:].rearrange("p n t -> p (n t)"),
            )

        v_rows = {}
        v_grouped = {}
        v_codes = keep.tile([P, PASSES, N], U32, name="v_codes", align_bytes=64)
        v_scales = keep.tile([P, PASSES, N], U8, name="v_scales", align_bytes=64)

        def stage_one(h, s):
            cols = slice(h * HALF, (h + 1) * HALF)
            v_rows[h, s] = long_work.tile([P, PACK, HALF], BF16, name="v_rows")
            for t in range(PACK):
                v_acc = psum_acc.tile([P, HALF], F32, name="v_acc", tag="acc")
                for g in range(PASSES):
                    nc.tensor.matmul_mx(
                        out=v_acc[:],
                        lhsT=wv_codes[s][:, t, g].bitcast(FP8X4),
                        lhsT_scale=wv_scales[s][:, t, g],
                        rhs=xm_codes[:, g, cols].bitcast(FP8X4),
                        rhs_scale=xm_scales[:, g, cols],
                        start=(g == 0),
                        stop=(g == PASSES - 1),
                    )
                nc.scalar.activation(
                    out=v_rows[h, s][:, t, :],
                    in_=v_acc[:],
                    func=ACT.Identity,
                    bias=bias[:, s * PACK + t : s * PACK + t + 1],
                    scale=1.0,
                )

        def regroup_v(h, s):
            v_grouped[h, s] = work.tile([P, HALF, PACK], BF16, name="v_grouped", align_bytes=64)
            regroup(v_grouped[h, s][:], v_rows[h, s][:])

        def quantise_v(h, s):
            cols = slice(h * HALF, (h + 1) * HALF)
            nc.vector.quantize_mx(
                out=v_codes[:, s, cols].bitcast(FP8X4),
                scales=v_scales[:, s, cols],
                in_=v_grouped[h, s][:].rearrange("p n t -> p (n t)"),
            )

        neg_max = const.tile([P, MAPS * ROW_TILES], F32, name="neg_max")
        row_sum = const.tile([P, MAPS * ROW_TILES], F32, name="row_sum")
        inv_sum = const.tile([P, MAPS * ROW_TILES], F32, name="inv_sum")
        expo = {}
        att = {}
        turned_att = {}
        att_grouped = {}
        att_codes = {}
        att_scales = {}

        def row_max(r, i):
            expo[r, i] = long_work.tile([P, C], F32, name="expo")
            nc.vector.tensor_scalar(
                out=expo[r, i][:, 0 : C // 2].bitcast(BF16),
                in0=score_sb[r, i][:],
                scalar1=-1.0,
                scalar2=None,
                op0=ALU.mult,
                op1=ALU.min,
                accum_out=neg_max[:, MAPS * r + i : MAPS * r + i + 1],
            )

        def exponentials(r):
            for i in range(MAPS):
                col = slice(MAPS * r + i, MAPS * r + i + 1)
                nc.scalar.activation(
                    out=expo[r, i][:],
                    in_=score_sb[r, i][:],
                    func=ACT.Exp,
                    bias=neg_max[:, col],
                    scale=1.0,
                    accum_out=row_sum[:, col],
                )

        def reciprocal(r, i):
            col = slice(MAPS * r + i, MAPS * r + i + 1)
            nc.vector.reciprocal(out=inv_sum[:, col], in_=row_sum[:, col])

        def scale_by_scalar(r, i):
            att[r, i] = work.tile([P, C], BF16, name="att")
            nc.scalar.activation(
                out=att[r, i][:], in_=expo[r, i][:], func=ACT.Copy,
                scale=inv_sum[:, MAPS * r + i : MAPS * r + i + 1],
            )

        def scale(r, maps=range(MAPS)):
            for i in maps:
                att[r, i] = work.tile([P, C], BF16, name="att")
                nc.vector.tensor_scalar(
                    out=att[r, i][:], in0=expo[r, i][:],
                    scalar1=inv_sum[:, MAPS * r + i : MAPS * r + i + 1], scalar2=None, op0=ALU.mult,
                )

        def turn(r):
            for i in range(MAPS):
                att_words = att[r, i][:].bitcast(F32)
                turned_att[r, i] = psum_turn.tile([P, PASSES, 2, P], F32, name="turned")
                for g in range(PASSES):
                    for u in range(2):
                        first = (2 * g + u) * P
                        nc.tensor.transpose(
                            turned_att[r, i][:, g, u, :], att_words[:, first : first + P], ident[:]
                        )

        def copy_att(r):
            att_grouped[r] = work.tile([P, MAPS * C], BF16, name="att_grouped", align_bytes=64)
            grouped_words = att_grouped[r][:].bitcast(F32).rearrange(
                "p (i g c u) -> p i g c u", i=MAPS, g=PASSES, u=2
            )
            for i in range(MAPS):
                nc.scalar.copy(
                    out=grouped_words[:, i], in_=turned_att[r, i][:].rearrange("p g u c -> p g c u")
                )

        def quantise_att(r):
            att_codes[r] = keep.tile([P, MAPS * PASSES * P], U32, name="att_codes%d" % r, align_bytes=64)
            att_scales[r] = keep.tile([P, MAPS * PASSES * P], U8, name="att_scales%d" % r, align_bytes=64)
            nc.vector.quantize_mx(
                out=att_codes[r][:].bitcast(FP8X4), scales=att_scales[r][:], in_=att_grouped[r][:]
            )

        mean_acc = {}
        mean = {}
        o_acc = {}

        def add_frames(r):
            for h in range(HALVES):
                cols = slice(h * HALF, (h + 1) * HALF)
                mean_acc[r, h] = psum_mean.tile([P, HALF], F32, name="mean_acc")
                nc.tensor.matmul(
                    out=mean_acc[r, h][:], lhsT=half_ident[:], rhs=xl_sb[r // PACK][:, r % PACK, cols],
                    start=True, stop=False,
                )
                nc.tensor.matmul(
                    out=mean_acc[r, h][:], lhsT=half_ident[:], rhs=xf_sb[r // PACK][:, r % PACK, cols],
                    start=False, stop=True,
                )

        def vector_mean(r):
            a, b = r // PACK, r % PACK
            mean[r] = work.tile([P, N], F32, name="mean")
            nc.vector.tensor_scalar(
                out=xf_sb[a][:, b, :], in0=xf_sb[a][:, b, :], scalar1=0.5, scalar2=None, op0=ALU.mult
            )
            nc.vector.scalar_tensor_tensor(
                out=mean[r][:], in0=xl_sb[a][:, b, :], scalar=0.5, in1=xf_sb[a][:, b, :],
                op0=ALU.mult, op1=ALU.add,
            )

        def copy_mean(r):
            mean[r] = work.tile([P, N], F32, name="mean")
            for h in range(HALVES):
                nc.scalar.copy(out=mean[r][:, h * HALF : (h + 1) * HALF], in_=mean_acc[r, h][:])

        def pieces(r):
            if r < ROW_TILES - 1:
                return [slice(0, HALF), slice(HALF, N)]
            return [slice(0, HALF), slice(HALF, HALF + HALF // 2), slice(HALF + HALF // 2, N)]

        def stage_two(r):
            for h, cols in enumerate(pieces(r)):
                o_acc[r, h] = psum_acc.tile([P, cols.stop - cols.start], F32, name="o_acc", tag="acc")
                for i in range(MAPS):
                    for g in range(PASSES):
                        block = slice((i * PASSES + g) * P, (i * PASSES + g + 1) * P)
                        nc.tensor.matmul_mx(
                            out=o_acc[r, h][:],
                            lhsT=att_codes[r][:, block].bitcast(FP8X4),
                            lhsT_scale=att_scales[r][:, block],
                            rhs=v_codes[:, g, cols].bitcast(FP8X4),
                            rhs_scale=v_scales[:, g, cols],
                            start=(i == 0 and g == 0),
                            stop=(i == MAPS - 1 and g == PASSES - 1),
                        )

        def fuse_and_store(r, h):
            cols = pieces(r)[h]
            result = long_work.tile([P, cols.stop - cols.start], F32, name="result")
            nc.vector.scalar_tensor_tensor(
                out=result[:], in0=o_acc[r, h][:], scalar=gain[:, 0:1], in1=mean[r][:, cols],
                op0=ALU.mult, op1=ALU.add,
            )
            nc.sync.dma_start(out=out[r * P : (r + 1) * P, cols], in_=result[:])

        with tc.manual_schedule():
            row_max(0, 0)
            row_max(0, 1)
            exponentials(0)
            spread_small()
            turn_wv(0, (0, 1))
            row_max(1, 0)
            row_max(1, 1)
            exponentials(1)
            reciprocal(0, 0)
            reciprocal(0, 1)
            scale(0)
            quantise_wv(0, 0, 2)
            turn(0)
            regroup_xm(0, 0)
            reciprocal(1, 0)
            reciprocal(1, 1)
            regroup_xm(1, 0)
            copy_att(0)
            scale_by_scalar(1, 0)
            turn_wv(0, (2, 3))
            quantise_xm(0, 0)
            quantise_xm(1, 0)
            turn_wv(1)
            regroup_xm(0, 1)
            quantise_wv(0, 2, 2)
            regroup_xm(1, 1)
            quantise_xm(0, 1)
            quantise_xm(1, 1)
            load_frames()
            stage_one(0, 0)
            stage_one(1, 0)
            quantise_wv(1)
            scale(1, (1,))
            stage_one(0, 1)
            stage_one(1, 1)
            row_max(FIRST, 0)
            row_max(FIRST, 1)
            regroup_v(0, 0)
            regroup_v(1, 0)
            quantise_v(0, 0)
            regroup_v(0, 1)
            quantise_v(1, 0)
            regroup_v(1, 1)
            quantise_v(0, 1)
            quantise_att(0)
            quantise_v(1, 1)
            add_frames(0)
            copy_mean(0)
            turn(1)

            def exists(r):
                return 0 <= r < ROW_TILES

            for a in range(FIRST, ROW_TILES + 3):
                if exists(a):
                    exponentials(a)
                if exists(a - 1) and a - 1 < LAST:
                    add_frames(a - 1)
                if exists(a - 2):
                    stage_two(a - 2)
                if exists(a + 1):
                    row_max(a + 1, 0)
                if exists(a - 3):
                    fuse_and_store(a - 3, 0)
                if exists(a + 1):
                    row_max(a + 1, 1)
                if a == LAST:
                    vector_mean(a)
                if exists(a):
                    reciprocal(a, 0)
                if exists(a - 3):
                    for h in range(1, len(pieces(a - 3))):
                        fuse_and_store(a - 3, h)
                if exists(a - 1):
                    copy_att(a - 1)
                    if a - 1 < LAST:
                        copy_mean(a - 1)
                if exists(a):
                    reciprocal(a, 1)
                    scale(a)
                if exists(a - 1):
                    quantise_att(a - 1)
                if exists(a):
                    turn(a)
